import numpy as np
import ml_dtypes


def mxq(x, axis, fmt="e4m3"):
    dtype, down = {"e4m3": (ml_dtypes.float8_e4m3fn, 7), "e5m2": (ml_dtypes.float8_e5m2, 14)}[fmt]
    v = np.moveaxis(np.asarray(x, np.float32).astype(ml_dtypes.bfloat16).astype(np.float64), axis, -1)
    blocks = v.reshape(v.shape[:-1] + (-1, 32))
    amax = np.abs(blocks).max(-1, keepdims=True)
    byte = np.maximum(np.where(amax > 0, np.frexp(amax)[1] - 1 + 127, 0) - down, 1)
    scale = np.exp2(byte - 127.0)
    codes = (blocks / scale).astype(np.float32).astype(dtype).astype(np.float64)
    return np.moveaxis((codes * scale).reshape(v.shape), -1, axis)


WIDE = False


def mx_kscale(k):
    if not WIDE:
        return np.ones(k)
    levels = np.array([10, -10, 5, -5, 0])
    a = np.random.permutation(np.resize(levels, k // 512 * 4)).reshape(k // 512, 4)
    idx = np.arange(k)
    return np.exp2(a[idx // 512, idx % 128 // 32])


BF16 = ml_dtypes.bfloat16


def bf(x):
    return np.asarray(x, np.float32).astype(BF16)


def f64(x):
    return np.asarray(x).astype(np.float64)


B, T, D, N, L, H = 128, 16, 1024, 77, 512, 16
EPS = 1e-5


def silu(v):
    e = np.exp(-np.abs(v))
    return v * np.where(v >= 0.0, 1.0, e) / (1.0 + e)


def layer_norm(v, g, b):
    m = v.mean(-1, keepdims=True)
    var = ((v - m) ** 2).mean(-1, keepdims=True)
    return (v - m) / np.sqrt(var + EPS) * g + b


def setup_inputs():
    r = np.random.standard_normal
    s = mx_kscale(D)
    su = s / s.min()
    return {
        "x": bf(r((B, T, D))),
        "y": bf(r((B, T, D)) * 0.25),
        "emb0": bf(r((B, D)) * su),
        "We": bf(r((D, 2 * D)) / np.sqrt(D) / su[:, None]),
        "be": bf(r(2 * D) * 0.1),
        "ln2_g": bf(1.0 + 0.1 * r(D)),
        "ln2_b": bf(r(D) * 0.1),
        "Wo": bf(r((D, D)) / np.sqrt(D)),
        "bo": bf(r(D) * 0.1),
    }


def reference(x, y, emb0, We, be, ln2_g, ln2_b, Wo, bo):
    emb_out = (mxq(silu(f64(emb0)), 1, "e4m3") @ mxq(f64(We), 0, "e4m3")) + f64(be)
    scale, shift = emb_out[:, None, :D], emb_out[:, None, D:]
    h = layer_norm(f64(y), f64(ln2_g), f64(ln2_b)) * (1.0 + scale) + shift
    a = silu(h)
    return f64(x) + ((mxq(a, 2, "e4m3") @ mxq(f64(Wo), 0, "e4m3")) + f64(bo))

@@ -1,0 +1,328 @@
+from contextlib import ExitStack
+
+import concourse.mybir as mybir
+from concourse.masks import make_identity
+
+F32 = mybir.dt.float32
+BF16 = mybir.dt.bfloat16
+I32 = mybir.dt.int32
+U32 = mybir.dt.uint32
+U8 = mybir.dt.uint8
+FP8X4 = mybir.dt.float8_e4m3fn_x4
+ACT = mybir.ActivationFunctionType
+ALU = mybir.AluOpType
+
+P = 128
+T = 16
+D = 1024
+EPS = 1e-5
+PACK = 4
+K_PASS = P * PACK
+PASSES = D // K_PASS
+CHUNKS = D // P
+BANK = 512
+HALVES = D // BANK
+W_COLS = 1024
+LOAD_TILES = 4
+BN_MAX = 512
+BN_DIM = 6
+
+FLOPS = 2 * P * D * (2 * D) + 2 * (P * T) * D * D
+
+
+def load_weight_piece(nc, pool, rows):
+    raw = pool.tile([P, PACK, W_COLS], BF16)
+    nc.sync.dma_start(out=raw[:], in_=rows.rearrange("(j p) n -> p j n", p=P))
+    return raw
+
+
+def regroup_weight_piece(nc, pool, raw):
+    grouped = pool.tile([P, W_COLS, PACK], BF16, align_bytes=64)
+    first = slice(0, W_COLS // 2)
+    second = slice(W_COLS // 2, W_COLS)
+    nc.scalar.copy(
+        out=grouped[:, first, :].rearrange("p (c i) j -> p c j i", i=4),
+        in_=raw[:, :, first].rearrange("p j (c i) -> p c j i", i=4),
+    )
+    nc.gpsimd.tensor_scalar(
+        out=grouped[:, second, :],
+        in0=raw[:, :, second].rearrange("p j n -> p n j"),
+        scalar1=1.0,
+        scalar2=0.0,
+        op0=ALU.mult,
+        op1=ALU.add,
+    )
+    return grouped
+
+
+def quantise(nc, grouped_flat, codes, scales):
+    nc.vector.quantize_mx(out=codes.bitcast(FP8X4), scales=scales, in_=grouped_flat)
+
+
+def transpose_rows(nc, psum, rows, addend, ident):
+    banks = []
+    for g in range(PASSES):
+        bank = psum.tile([P, PACK, P], F32, tag="kT", name="kT")
+        for j in range(PACK):
+            cols = slice((PACK * g + j) * P, (PACK * g + j + 1) * P)
+            if addend is None:
+                nc.tensor.transpose(out=bank[:, j, :], in_=rows[:, cols], identity=ident[:])
+            else:
+                nc.tensor.matmul(
+                    out=bank[:, j, :], lhsT=addend[:, cols], rhs=ident[:],
+                    is_transpose=True, start=True, stop=False,
+                )
+                nc.tensor.matmul(
+                    out=bank[:, j, :], lhsT=rows[:, cols], rhs=ident[:],
+                    is_transpose=True, start=False, stop=True,
+                )
+        banks.append(bank)
+    return banks
+
+
+def silu_out_of_psum(nc, pool, banks):
+    grouped = pool.tile([P, PASSES, P, PACK], BF16, align_bytes=64, tag="act_grouped", name="act_grouped")
+    for g in range(PASSES):
+        nc.scalar.activation(
+            out=grouped[:, g, :, :], in_=banks[g][:].rearrange("p j r -> p r j"), func=ACT.Silu
+        )
+    return grouped
+
+
+def tile_temporalcrossattention_pa_kernel(tc, x, y, emb0, We, be, ln2_g, ln2_b, Wo, bo, out):
+    nc = tc.nc
+    with ExitStack() as ctx:
+        keep = ctx.enter_context(tc.tile_pool(name="keep", bufs=1))
+        we_raw_pool = ctx.enter_context(tc.tile_pool(name="we_raw", bufs=2 * PASSES))
+        wo_raw_pool = ctx.enter_context(tc.tile_pool(name="wo_raw", bufs=PASSES))
+        w_grouped_pool = ctx.enter_context(tc.tile_pool(name="w_grouped", bufs=2))
+        z_pool = ctx.enter_context(tc.tile_pool(name="z", bufs=3))
+        act_pool = ctx.enter_context(tc.tile_pool(name="act", bufs=3))
+        res_pool = ctx.enter_context(tc.tile_pool(name="res", bufs=5))
+        small = ctx.enter_context(tc.tile_pool(name="small", bufs=4))
+        psum_keep = ctx.enter_context(tc.psum_pool(name="psum_keep", bufs=1))
+        psum_t = ctx.enter_context(tc.psum_pool(name="psum_t", bufs=3))
+        psum_mm = ctx.enter_context(tc.psum_pool(name="psum_mm", bufs=3))
+
+        ident = keep.tile([P, P], F32)
+        make_identity(nc, ident[:])
+        minus_half = keep.tile([P, LOAD_TILES], F32)
+        nc.gpsimd.memset(minus_half[:], -0.5)
+        vec_rows = keep.tile([P, P], BF16)
+        nc.vector.memset(vec_rows[:].bitcast(I32), 0)
+
+        emb_raw = keep.tile([P, D], BF16)
+        nc.sync.dma_start(out=emb_raw[:], in_=emb0)
+        nc.sync.dma_start(out=vec_rows[0:16, :], in_=be.rearrange("(r c) -> r c", c=P))
+        nc.sync.dma_start(out=vec_rows[16:24, :], in_=ln2_g.rearrange("(r c) -> r c", c=P))
+        nc.sync.dma_start(out=vec_rows[24:32, :], in_=ln2_b.rearrange("(r c) -> r c", c=P))
+        y_sb = []
+        we_raw = []
+        for c in range(T // LOAD_TILES):
+            y_part = keep.tile([P, LOAD_TILES, D], BF16, name="y%d" % c)
+            nc.sync.dma_start(out=y_part[:], in_=y[:, c * LOAD_TILES : (c + 1) * LOAD_TILES, :])
+            y_sb.append(y_part)
+            g = c % PASSES
+            side = c // PASSES
+            we_raw.append(
+                load_weight_piece(
+                    nc, we_raw_pool,
+                    We[g * K_PASS : (g + 1) * K_PASS, side * W_COLS : (side + 1) * W_COLS],
+                )
+            )
+        wo_raw = [
+            load_weight_piece(nc, wo_raw_pool, Wo[g * K_PASS : (g + 1) * K_PASS, :])
+            for g in range(PASSES)
+        ]
+        bo_rows = keep.tile([P, D], BF16)
+        nc.sync.dma_start(out=bo_rows[:], in_=bo.partition_broadcast(P))
+        x_sb = []
+        for c in range(T // LOAD_TILES):
+            x_part = keep.tile([P, LOAD_TILES, D], BF16, name="x%d" % c)
+            nc.sync.dma_start(out=x_part[:], in_=x[:, c * LOAD_TILES : (c + 1) * LOAD_TILES, :])
+            x_sb.append(x_part)
+
+        emb_f32 = z_pool.tile([P, D], F32, tag="z", name="emb_f32")
+        nc.vector.tensor_copy(out=emb_f32[:], in_=emb_raw[:])
+        emb_codes = keep.tile([P, PASSES, P], U32, align_bytes=64)
+        emb_scales = keep.tile([P, PASSES, P], U8, align_bytes=64)
+        emb_grouped = silu_out_of_psum(nc, act_pool, transpose_rows(nc, psum_t, emb_f32, None, ident))
+        quantise(
+            nc,
+            emb_grouped[:].rearrange("p g r j -> p (g r j)"),
+            emb_codes[:].rearrange("p g r -> p (g r)"),
+            emb_scales[:].rearrange("p g r -> p (g r)"),
+        )
+
+        vec_f32 = keep.tile([P, P], F32)
+        nc.vector.tensor_copy(out=vec_f32[:], in_=vec_rows[:])
+        vec_bank = psum_t.tile([P, PACK, P], F32, tag="kT", name="vec_bank")
+        nc.tensor.transpose(out=vec_bank[:, 0, :], in_=vec_f32[:], identity=ident[:])
+        vec_cols = keep.tile([P, 4 * CHUNKS], F32)
+        nc.vector.tensor_copy(out=vec_cols[:], in_=vec_bank[:, 0, 0 : 4 * CHUNKS])
+        be_scale = vec_cols[:, 0:CHUNKS]
+        be_shift = vec_cols[:, CHUNKS : 2 * CHUNKS]
+        gain = vec_cols[:, 2 * CHUNKS : 3 * CHUNKS]
+        beta = vec_cols[:, 3 * CHUNKS : 4 * CHUNKS]
+        a_bias = keep.tile([P, CHUNKS], F32)
+        nc.vector.scalar_tensor_tensor(
+            out=a_bias[:], in0=be_scale, scalar=1.0, in1=gain, op0=ALU.add, op1=ALU.mult
+        )
+        c_bias = keep.tile([P, CHUNKS], F32)
+        nc.vector.scalar_tensor_tensor(
+            out=c_bias[:], in0=be_scale, scalar=1.0, in1=beta, op0=ALU.add, op1=ALU.mult
+        )
+        nc.vector.tensor_tensor(out=c_bias[:], in0=c_bias[:], in1=be_shift, op=ALU.add)
+
+        we_codes = keep.tile([P, 2 * PASSES, W_COLS], U32, align_bytes=64)
+        we_scales = keep.tile([P, 2 * PASSES, W_COLS], U8, align_bytes=64)
+        wo_codes = keep.tile([P, PASSES, W_COLS], U32, align_bytes=64)
+        wo_scales = keep.tile([P, PASSES, W_COLS], U8, align_bytes=64)
+        mean_var = keep.tile([P, T, 2], F32)
+        rstd = keep.tile([P, T], F32)
+        z_bias = keep.tile([P, T], F32)
+        for c in range(T // LOAD_TILES):
+            we_grouped = regroup_weight_piece(nc, w_grouped_pool, we_raw[c])
+            tiles = slice(c * LOAD_TILES, (c + 1) * LOAD_TILES)
+            for i in range(LOAD_TILES):
+                stats = small.tile([P, D // BN_MAX, BN_DIM], F32)
+                for s in range(D // BN_MAX):
+                    nc.vector.bn_stats(
+                        out=stats[:, s, :], in_=y_sb[c][:, i, s * BN_MAX : (s + 1) * BN_MAX]
+                    )
+                nc.vector.bn_aggr(
+                    out=mean_var[:, c * LOAD_TILES + i, :], in_=stats[:].rearrange("p s k -> p (s k)")
+                )
+            var_eps = small.tile([P, LOAD_TILES], F32)
+            nc.gpsimd.tensor_scalar(
+                out=var_eps[:], in0=mean_var[:, tiles, 1], scalar1=1.0, scalar2=EPS,
+                op0=ALU.mult, op1=ALU.add,
+            )
+            nc.gpsimd.tensor_tensor(out=rstd[:, tiles], in0=var_eps[:], in1=minus_half[:], op=ALU.pow)
+            neg_mean = small.tile([P, LOAD_TILES], F32)
+            nc.gpsimd.tensor_scalar(
+                out=neg_mean[:], in0=mean_var[:, tiles, 0], scalar1=-1.0, scalar2=0.0,
+                op0=ALU.mult, op1=ALU.add,
+            )
+            nc.gpsimd.tensor_tensor(out=z_bias[:, tiles], in0=neg_mean[:], in1=rstd[:, tiles], op=ALU.mult)
+            quantise(
+                nc, we_grouped[:].rearrange("p n j -> p (n j)"), we_codes[:, c, :], we_scales[:, c, :]
+            )
+        for g in range(PASSES):
+            wo_grouped = regroup_weight_piece(nc, w_grouped_pool, wo_raw[g])
+            quantise(
+                nc, wo_grouped[:].rearrange("p n j -> p (n j)"), wo_codes[:, g, :], wo_scales[:, g, :]
+            )
+
+        a_t = res_pool.tile([P, CHUNKS, P], F32, tag="res", name="a_t")
+        l_t = res_pool.tile([P, CHUNKS, P], F32, tag="res", name="l_t")
+        c_t = res_pool.tile([P, CHUNKS, P], F32, tag="res", name="c_t")
+        c_rows = keep.tile([P, D], F32)
+        a_banks = []
+        for h in range(HALVES):
+            e_banks = []
+            for side in range(2):
+                e_bank = psum_mm.tile([P, PACK, P], F32, tag="mm", name="e_bank")
+                for i in range(PACK):
+                    cols = slice(h * BANK + i * P, h * BANK + (i + 1) * P)
+                    for g in range(PASSES):
+                        nc.tensor.matmul_mx(
+                            out=e_bank[:, i, :],
+                            lhsT=we_codes[:, side * PASSES + g, cols].bitcast(FP8X4),
+                            lhsT_scale=we_scales[:, side * PASSES + g, cols],
+                            rhs=emb_codes[:, g, :].bitcast(FP8X4),
+                            rhs_scale=emb_scales[:, g, :],
+                            start=(g == 0),
+                            stop=(g == PASSES - 1),
+                        )
+                e_banks.append(e_bank)
+            for i in range(PACK):
+                k = h * PACK + i
+                nc.scalar.activation(
+                    out=a_t[:, k, :], in_=e_banks[0][:, i, :], func=ACT.Identity,
+                    scale=gain[:, k : k + 1], bias=a_bias[:, k : k + 1],
+                )
+                nc.scalar.activation(
+                    out=l_t[:, k, :], in_=e_banks[0][:, i, :], func=ACT.Identity,
+                    scale=beta[:, k : k + 1], bias=c_bias[:, k : k + 1],
+                )
+            chunks = slice(h * PACK, (h + 1) * PACK)
+            nc.vector.tensor_tensor(out=c_t[:, chunks, :], in0=e_banks[1][:], in1=l_t[:, chunks, :], op=ALU.add)
+            a_bank = psum_keep.tile([P, PACK, P], F32, name="a_bank%d" % h)
+            c_bank = psum_t.tile([P, PACK, P], F32, tag="kT", name="c_bank")
+            for i in range(PACK):
+                nc.tensor.transpose(out=a_bank[:, i, :], in_=a_t[:, h * PACK + i, :], identity=ident[:])
+                nc.tensor.transpose(out=c_bank[:, i, :], in_=c_t[:, h * PACK + i, :], identity=ident[:])
+            nc.scalar.copy(
+                out=c_rows[:, h * BANK : (h + 1) * BANK], in_=c_bank[:].rearrange("p i d -> p (i d)")
+            )
+            a_banks.append(a_bank)
+
+        z_tiles = {}
+        h_banks = {}
+        act_codes = {}
+        act_scales = {}
+        residual = {}
+
+        def normalise(t):
+            z = z_pool.tile([P, D], F32, tag="z", name="z")
+            nc.scalar.activation(
+                out=z[:], in_=y_sb[t // LOAD_TILES][:, t % LOAD_TILES, :], func=ACT.Identity,
+                scale=rstd[:, t : t + 1], bias=z_bias[:, t : t + 1],
+            )
+            z_tiles[t] = z
+
+        def modulate_and_transpose(t):
+            z = z_tiles[t]
+            for h in range(HALVES):
+                cols = slice(h * BANK, (h + 1) * BANK)
+                nc.vector.tensor_tensor(
+                    out=z[:, cols], in0=z[:, cols], in1=a_banks[h][:].rearrange("p i d -> p (i d)"),
+                    op=ALU.mult,
+                )
+            h_banks[t] = transpose_rows(nc, psum_t, z, c_rows, ident)
+
+        def residual_plus_bias(t):
+            res = res_pool.tile([P, D], F32, tag="res", name="res")
+            nc.gpsimd.tensor_tensor(
+                out=res[:], in0=x_sb[t // LOAD_TILES][:, t % LOAD_TILES, :], in1=bo_rows[:], op=ALU.add
+            )
+            residual[t] = res
+
+        def activate_and_quantise(t):
+            grouped = silu_out_of_psum(nc, act_pool, h_banks[t])
+            codes = act_pool.tile([P, PASSES, P], U32, align_bytes=64, tag="act_codes", name="act_codes")
+            scales = act_pool.tile([P, PASSES, P], U8, align_bytes=64, tag="act_scales", name="act_scales")
+            quantise(
+                nc,
+                grouped[:].rearrange("p g r j -> p (g r j)"),
+                codes[:].rearrange("p g r -> p (g r)"),
+                scales[:].rearrange("p g r -> p (g r)"),
+            )
+            act_codes[t] = codes
+            act_scales[t] = scales
+
+        def project_and_store(t):
+            res = residual[t]
+            for h in range(HALVES):
+                cols = slice(h * BANK, (h + 1) * BANK)
+                acc = psum_mm.tile([P, BANK], F32, tag="mm", name="acc")
+                for g in range(PASSES):
+                    nc.tensor.matmul_mx(
+                        out=acc[:],
+                        lhsT=act_codes[t][:, g, :].bitcast(FP8X4),
+                        lhsT_scale=act_scales[t][:, g, :],
+                        rhs=wo_codes[:, g, cols].bitcast(FP8X4),
+                        rhs_scale=wo_scales[:, g, cols],
+                        start=(g == 0),
+                        stop=(g == PASSES - 1),
+                    )
+                nc.vector.tensor_tensor(out=res[:, cols], in0=acc[:], in1=res[:, cols], op=ALU.add)
+            nc.sync.dma_start(out=out[:, t, :], in_=res[:])
+
+        for t in range(T):
+            normalise(t)
+            residual_plus_bias(t)
+            modulate_and_transpose(t)
+            activate_and_quantise(t)
+            project_and_store(t)

@@ -100,9 +100,10 @@ def tile_temporalcrossattention_pa_kernel(tc, x, y, emb0, We, be, ln2_g, ln2_b, 
         act_pool = ctx.enter_context(tc.tile_pool(name="act", bufs=3))
         res_pool = ctx.enter_context(tc.tile_pool(name="res", bufs=5))
         small = ctx.enter_context(tc.tile_pool(name="small", bufs=4))
-        psum_keep = ctx.enter_context(tc.psum_pool(name="psum_keep", bufs=1))
+        psum_keep = ctx.enter_context(tc.psum_pool(name="psum_keep", bufs=HALVES))
         psum_t = ctx.enter_context(tc.psum_pool(name="psum_t", bufs=3))
         psum_mm = ctx.enter_context(tc.psum_pool(name="psum_mm", bufs=3))
+        ctx.enter_context(tc.manual_schedule())
 
         ident = keep.tile([P, P], F32)
         make_identity(nc, ident[:])
@@ -111,6 +112,11 @@ def tile_temporalcrossattention_pa_kernel(tc, x, y, emb0, We, be, ln2_g, ln2_b, 
         vec_rows = keep.tile([P, P], BF16)
         nc.vector.memset(vec_rows[:].bitcast(I32), 0)
 
+        def load_tiles(src, c, name):
+            part = keep.tile([P, LOAD_TILES, D], BF16, name=name % c)
+            nc.sync.dma_start(out=part[:], in_=src[:, c * LOAD_TILES : (c + 1) * LOAD_TILES, :])
+            return part
+
         emb_raw = keep.tile([P, D], BF16)
         nc.sync.dma_start(out=emb_raw[:], in_=emb0)
         nc.sync.dma_start(out=vec_rows[0:16, :], in_=be.rearrange("(r c) -> r c", c=P))
@@ -118,29 +124,24 @@ def tile_temporalcrossattention_pa_kernel(tc, x, y, emb0, We, be, ln2_g, ln2_b, 
         nc.sync.dma_start(out=vec_rows[24:32, :], in_=ln2_b.rearrange("(r c) -> r c", c=P))
         y_sb = []
         we_raw = []
-        for c in range(T // LOAD_TILES):
-            y_part = keep.tile([P, LOAD_TILES, D], BF16, name="y%d" % c)
-            nc.sync.dma_start(out=y_part[:], in_=y[:, c * LOAD_TILES : (c + 1) * LOAD_TILES, :])
-            y_sb.append(y_part)
-            g = c % PASSES
-            side = c // PASSES
-            we_raw.append(
-                load_weight_piece(
-                    nc, we_raw_pool,
-                    We[g * K_PASS : (g + 1) * K_PASS, side * W_COLS : (side + 1) * W_COLS],
+        for side in range(2):
+            y_sb.append(load_tiles(y, side, "y%d"))
+            for g in range(PASSES):
+                we_raw.append(
+                    load_weight_piece(
+                        nc, we_raw_pool,
+                        We[g * K_PASS : (g + 1) * K_PASS, side * W_COLS : (side + 1) * W_COLS],
+                    )
                 )
-            )
+        for c in range(2, T // LOAD_TILES):
+            y_sb.append(load_tiles(y, c, "y%d"))
         wo_raw = [
             load_weight_piece(nc, wo_raw_pool, Wo[g * K_PASS : (g + 1) * K_PASS, :])
             for g in range(PASSES)
         ]
         bo_rows = keep.tile([P, D], BF16)
         nc.sync.dma_start(out=bo_rows[:], in_=bo.partition_broadcast(P))
-        x_sb = []
-        for c in range(T // LOAD_TILES):
-            x_part = keep.tile([P, LOAD_TILES, D], BF16, name="x%d" % c)
-            nc.sync.dma_start(out=x_part[:], in_=x[:, c * LOAD_TILES : (c + 1) * LOAD_TILES, :])
-            x_sb.append(x_part)
+        x_sb = [load_tiles(x, c, "x%d") for c in range(T // LOAD_TILES)]
 
         emb_f32 = z_pool.tile([P, D], F32, tag="z", name="emb_f32")
         nc.vector.tensor_copy(out=emb_f32[:], in_=emb_raw[:])
@@ -174,18 +175,13 @@ def tile_temporalcrossattention_pa_kernel(tc, x, y, emb0, We, be, ln2_g, ln2_b, 
         )
         nc.vector.tensor_tensor(out=c_bias[:], in0=c_bias[:], in1=be_shift, op=ALU.add)
 
-        we_codes = keep.tile([P, 2 * PASSES, W_COLS], U32, align_bytes=64)
-        we_scales = keep.tile([P, 2 * PASSES, W_COLS], U8, align_bytes=64)
-        wo_codes = keep.tile([P, PASSES, W_COLS], U32, align_bytes=64)
-        wo_scales = keep.tile([P, PASSES, W_COLS], U8, align_bytes=64)
         mean_var = keep.tile([P, T, 2], F32)
         rstd = keep.tile([P, T], F32)
         z_bias = keep.tile([P, T], F32)
-        for c in range(T // LOAD_TILES):
-            we_grouped = regroup_weight_piece(nc, w_grouped_pool, we_raw[c])
-            tiles = slice(c * LOAD_TILES, (c + 1) * LOAD_TILES)
+
+        def row_moments(c):
             for i in range(LOAD_TILES):
-                stats = small.tile([P, D // BN_MAX, BN_DIM], F32)
+                stats = small.tile([P, D // BN_MAX, BN_DIM], F32, name="stats")
                 for s in range(D // BN_MAX):
                     nc.vector.bn_stats(
                         out=stats[:, s, :], in_=y_sb[c][:, i, s * BN_MAX : (s + 1) * BN_MAX]
@@ -193,35 +189,39 @@ def tile_temporalcrossattention_pa_kernel(tc, x, y, emb0, We, be, ln2_g, ln2_b, 
                 nc.vector.bn_aggr(
                     out=mean_var[:, c * LOAD_TILES + i, :], in_=stats[:].rearrange("p s k -> p (s k)")
                 )
-            var_eps = small.tile([P, LOAD_TILES], F32)
+
+        def row_scales(c):
+            tiles = slice(c * LOAD_TILES, (c + 1) * LOAD_TILES)
+            var_eps = small.tile([P, LOAD_TILES], F32, name="var_eps")
             nc.gpsimd.tensor_scalar(
                 out=var_eps[:], in0=mean_var[:, tiles, 1], scalar1=1.0, scalar2=EPS,
                 op0=ALU.mult, op1=ALU.add,
             )
             nc.gpsimd.tensor_tensor(out=rstd[:, tiles], in0=var_eps[:], in1=minus_half[:], op=ALU.pow)
-            neg_mean = small.tile([P, LOAD_TILES], F32)
+            neg_mean = small.tile([P, LOAD_TILES], F32, name="neg_mean")
             nc.gpsimd.tensor_scalar(
                 out=neg_mean[:], in0=mean_var[:, tiles, 0], scalar1=-1.0, scalar2=0.0,
                 op0=ALU.mult, op1=ALU.add,
             )
             nc.gpsimd.tensor_tensor(out=z_bias[:, tiles], in0=neg_mean[:], in1=rstd[:, tiles], op=ALU.mult)
-            quantise(
-                nc, we_grouped[:].rearrange("p n j -> p (n j)"), we_codes[:, c, :], we_scales[:, c, :]
-            )
-        for g in range(PASSES):
-            wo_grouped = regroup_weight_piece(nc, w_grouped_pool, wo_raw[g])
-            quantise(
-                nc, wo_grouped[:].rearrange("p n j -> p (n j)"), wo_codes[:, g, :], wo_scales[:, g, :]
-            )
 
-        a_t = res_pool.tile([P, CHUNKS, P], F32, tag="res", name="a_t")
-        l_t = res_pool.tile([P, CHUNKS, P], F32, tag="res", name="l_t")
-        c_t = res_pool.tile([P, CHUNKS, P], F32, tag="res", name="c_t")
-        c_rows = keep.tile([P, D], F32)
-        a_banks = []
-        for h in range(HALVES):
-            e_banks = []
-            for side in range(2):
+        we_codes = keep.tile([P, 2 * PASSES, W_COLS], U32, align_bytes=64)
+        we_scales = keep.tile([P, 2 * PASSES, W_COLS], U8, align_bytes=64)
+        for side in range(2):
+            row_moments(side)
+            for g in range(PASSES):
+                c = side * PASSES + g
+                we_grouped = regroup_weight_piece(nc, w_grouped_pool, we_raw[c])
+                quantise(
+                    nc, we_grouped[:].rearrange("p n j -> p (n j)"), we_codes[:, c, :], we_scales[:, c, :]
+                )
+            row_scales(side)
+
+        a_t = res_pool.tile([P, D], F32, tag="res", name="a_t")
+        l_t = res_pool.tile([P, D], F32, tag="res", name="l_t")
+        s_t = res_pool.tile([P, D], F32, tag="res", name="s_t")
+        for side in range(2):
+            for h in range(HALVES):
                 e_bank = psum_mm.tile([P, PACK, P], F32, tag="mm", name="e_bank")
                 for i in range(PACK):
                     cols = slice(h * BANK + i * P, h * BANK + (i + 1) * P)
@@ -235,34 +235,56 @@ def tile_temporalcrossattention_pa_kernel(tc, x, y, emb0, We, be, ln2_g, ln2_b, 
                             start=(g == 0),
                             stop=(g == PASSES - 1),
                         )
-                e_banks.append(e_bank)
-            for i in range(PACK):
-                k = h * PACK + i
-                nc.scalar.activation(
-                    out=a_t[:, k, :], in_=e_banks[0][:, i, :], func=ACT.Identity,
-                    scale=gain[:, k : k + 1], bias=a_bias[:, k : k + 1],
-                )
-                nc.scalar.activation(
-                    out=l_t[:, k, :], in_=e_banks[0][:, i, :], func=ACT.Identity,
-                    scale=beta[:, k : k + 1], bias=c_bias[:, k : k + 1],
-                )
-            chunks = slice(h * PACK, (h + 1) * PACK)
-            nc.vector.tensor_tensor(out=c_t[:, chunks, :], in0=e_banks[1][:], in1=l_t[:, chunks, :], op=ALU.add)
-            a_bank = psum_keep.tile([P, PACK, P], F32, name="a_bank%d" % h)
-            c_bank = psum_t.tile([P, PACK, P], F32, tag="kT", name="c_bank")
-            for i in range(PACK):
-                nc.tensor.transpose(out=a_bank[:, i, :], in_=a_t[:, h * PACK + i, :], identity=ident[:])
-                nc.tensor.transpose(out=c_bank[:, i, :], in_=c_t[:, h * PACK + i, :], identity=ident[:])
+                for i in range(PACK):
+                    k = h * PACK + i
+                    cols = slice(k * P, (k + 1) * P)
+                    if side == 0:
+                        nc.scalar.activation(
+                            out=a_t[:, cols], in_=e_bank[:, i, :], func=ACT.Identity,
+                            scale=gain[:, k : k + 1], bias=a_bias[:, k : k + 1],
+                        )
+                        nc.scalar.activation(
+                            out=l_t[:, cols], in_=e_bank[:, i, :], func=ACT.Identity,
+                            scale=beta[:, k : k + 1],
+                        )
+                    else:
+                        nc.scalar.activation(
+                            out=s_t[:, cols], in_=e_bank[:, i, :], func=ACT.Identity,
+                            bias=c_bias[:, k : k + 1],
+                        )
+        a_banks = transpose_rows(nc, psum_keep, a_t, None, ident)
+        c_banks = transpose_rows(nc, psum_t, s_t, l_t, ident)
+        c_rows = keep.tile([P, D], F32)
+        for h in range(HALVES):
             nc.scalar.copy(
-                out=c_rows[:, h * BANK : (h + 1) * BANK], in_=c_bank[:].rearrange("p i d -> p (i d)")
+                out=c_rows[:, h * BANK : (h + 1) * BANK], in_=c_banks[h][:].rearrange("p i d -> p (i d)")
             )
-            a_banks.append(a_bank)
+
+        wo_codes = keep.tile([P, PASSES, W_COLS], U32, align_bytes=64)
+        wo_scales = keep.tile([P, PASSES, W_COLS], U8, align_bytes=64)
+        wo_grouped = [regroup_weight_piece(nc, w_grouped_pool, wo_raw[g]) for g in range(PASSES)]
+        for c in range(2, T // LOAD_TILES):
+            row_moments(c)
+            row_scales(c)
+        for g in range(PASSES):
+            quantise(
+                nc, wo_grouped[g][:].rearrange("p n j -> p (n j)"), wo_codes[:, g, :], wo_scales[:, g, :]
+            )
 
         z_tiles = {}
         h_banks = {}
+        act_grouped = {}
         act_codes = {}
         act_scales = {}
+        products = {}
         residual = {}
+
+        def residual_plus_bias(t):
+            res = res_pool.tile([P, D], F32, tag="res", name="res")
+            nc.gpsimd.tensor_tensor(
+                out=res[:], in0=x_sb[t // LOAD_TILES][:, t % LOAD_TILES, :], in1=bo_rows[:], op=ALU.add
+            )
+            residual[t] = res
 
         def normalise(t):
             z = z_pool.tile([P, D], F32, tag="z", name="z")
@@ -282,28 +304,23 @@ def tile_temporalcrossattention_pa_kernel(tc, x, y, emb0, We, be, ln2_g, ln2_b, 
                 )
             h_banks[t] = transpose_rows(nc, psum_t, z, c_rows, ident)
 
-        def residual_plus_bias(t):
-            res = res_pool.tile([P, D], F32, tag="res", name="res")
-            nc.gpsimd.tensor_tensor(
-                out=res[:], in0=x_sb[t // LOAD_TILES][:, t % LOAD_TILES, :], in1=bo_rows[:], op=ALU.add
-            )
-            residual[t] = res
+        def activate(t):
+            act_grouped[t] = silu_out_of_psum(nc, act_pool, h_banks[t])
 
-        def activate_and_quantise(t):
-            grouped = silu_out_of_psum(nc, act_pool, h_banks[t])
+        def quantise_tile(t):
             codes = act_pool.tile([P, PASSES, P], U32, align_bytes=64, tag="act_codes", name="act_codes")
             scales = act_pool.tile([P, PASSES, P], U8, align_bytes=64, tag="act_scales", name="act_scales")
             quantise(
                 nc,
-                grouped[:].rearrange("p g r j -> p (g r j)"),
+                act_grouped[t][:].rearrange("p g r j -> p (g r j)"),
                 codes[:].rearrange("p g r -> p (g r)"),
                 scales[:].rearrange("p g r -> p (g r)"),
             )
             act_codes[t] = codes
             act_scales[t] = scales
 
-        def project_and_store(t):
-            res = residual[t]
+        def project(t):
+            products[t] = []
             for h in range(HALVES):
                 cols = slice(h * BANK, (h + 1) * BANK)
                 acc = psum_mm.tile([P, BANK], F32, tag="mm", name="acc")
@@ -317,12 +334,28 @@ def tile_temporalcrossattention_pa_kernel(tc, x, y, emb0, We, be, ln2_g, ln2_b, 
                         start=(g == 0),
                         stop=(g == PASSES - 1),
                     )
-                nc.vector.tensor_tensor(out=res[:, cols], in0=acc[:], in1=res[:, cols], op=ALU.add)
+                products[t].append(acc)
+
+        def finish(t):
+            res = residual[t]
+            for h in range(HALVES):
+                cols = slice(h * BANK, (h + 1) * BANK)
+                nc.vector.tensor_tensor(out=res[:, cols], in0=products[t][h][:], in1=res[:, cols], op=ALU.add)
             nc.sync.dma_start(out=out[:, t, :], in_=res[:])
 
-        for t in range(T):
-            normalise(t)
-            residual_plus_bias(t)
-            modulate_and_transpose(t)
-            activate_and_quantise(t)
-            project_and_store(t)
+        normalise(0)
+        for i in range(T + 2):
+            if i < T:
+                residual_plus_bias(i)
+            if 1 <= i <= T:
+                activate(i - 1)
+            if i + 1 < T:
+                normalise(i + 1)
+            if i < T:
+                modulate_and_transpose(i)
+            if 1 <= i <= T:
+                quantise_tile(i - 1)
+            if i >= 2:
+                finish(i - 2)
+            if 1 <= i <= T:
+                project(i - 1)

@@ -31,29 +31,27 @@ FLOPS = 2 * P * D * (2 * D) + 2 * (P * T) * D * D
 
 
 def load_weight_piece(nc, pool, rows):
-    raw = pool.tile([P, PACK, W_COLS], BF16)
+    raw = pool.tile([P, PACK, W_COLS], BF16, tag="raw", name="raw")
     nc.sync.dma_start(out=raw[:], in_=rows.rearrange("(j p) n -> p j n", p=P))
     return raw
 
 
-def regroup_weight_piece(nc, pool, raw):
-    grouped = pool.tile([P, W_COLS, PACK], BF16, align_bytes=64)
-    first = slice(0, W_COLS // 2)
-    second = slice(W_COLS // 2, W_COLS)
-    nc.scalar.copy(
-        out=grouped[:, first, :].rearrange("p (c i) j -> p c j i", i=4),
-        in_=raw[:, :, first].rearrange("p j (c i) -> p c j i", i=4),
-    )
-    nc.gpsimd.tensor_scalar(
-        out=grouped[:, second, :],
-        in0=raw[:, :, second].rearrange("p j n -> p n j"),
-        scalar1=1.0,
-        scalar2=0.0,
-        op0=ALU.mult,
-        op1=ALU.add,
-    )
-    return grouped
-
+def regroup(nc, grouped, raw, engine, lo, hi):
+    if engine == "G":
+        nc.gpsimd.tensor_scalar(
+            out=grouped[:],
+            in0=raw[:, :, lo:hi].rearrange("p j n -> p n j"),
+            scalar1=1.0,
+            scalar2=0.0,
+            op0=ALU.mult,
+            op1=ALU.add,
+        )
+    else:
+        copy = nc.scalar.copy if engine == "S" else nc.vector.tensor_copy
+        copy(
+            out=grouped[:].rearrange("p (c i) j -> p c j i", i=4),
+            in_=raw[:, :, lo:hi].rearrange("p j (c i) -> p c j i", i=4),
+        )
 
 def quantise(nc, grouped_flat, codes, scales):
     nc.vector.quantize_mx(out=codes.bitcast(FP8X4), scales=scales, in_=grouped_flat)
@@ -62,7 +60,7 @@ def quantise(nc, grouped_flat, codes, scales):
 def transpose_rows(nc, psum, rows, addend, ident):
     banks = []
     for g in range(PASSES):
-        bank = psum.tile([P, PACK, P], F32, tag="kT", name="kT")
+        bank = psum.tile([P, PACK, P], rows.dtype, tag="kT", name="kT")
         for j in range(PACK):
             cols = slice((PACK * g + j) * P, (PACK * g + j + 1) * P)
             if addend is None:
@@ -80,8 +78,8 @@ def transpose_rows(nc, psum, rows, addend, ident):
     return banks
 
 
-def silu_out_of_psum(nc, pool, banks):
-    grouped = pool.tile([P, PASSES, P, PACK], BF16, align_bytes=64, tag="act_grouped", name="act_grouped")
+def silu_out_of_psum(nc, pool, banks, tag="act_grouped"):
+    grouped = pool.tile([P, PASSES, P, PACK], BF16, align_bytes=64, tag=tag, name="act_grouped")
     for g in range(PASSES):
         nc.scalar.activation(
             out=grouped[:, g, :, :], in_=banks[g][:].rearrange("p j r -> p r j"), func=ACT.Silu
@@ -89,28 +87,34 @@ def silu_out_of_psum(nc, pool, banks):
     return grouped
 
 
+CFG = {"dma":["emb","e0","vec","e1","y0-2","e2","e3","y2-4","w0","w1","bo","x0-4","y4-8","x4-8","y8-12","y12-16","x8-12","x12-16"],"ops":[["ld","emb"],["tr_e"],["silu_e"],["ld","e0"],["pi","e0",512,768],["q_e"],["pe","e0","S",512,768,512,1024],["ld","vec"],["pi","e0",768,1024],["vec"],["pe","e0","S",768,1024,512,1024],["ld","e1"],["pi","e1",512,768],["rg","e0","V",0,512],["pe","e1","S",512,768,512,1024],["ld","y0-2"],["pi","e1",768,1024],["qw","e0",0,512],["pe","e1","S",768,1024,512,1024],["ld","e2"],["qw","e0",512,1024],["ld","e3"],["rg","e1","V",0,512],["ld","y2-4"],["qw","e1",0,512],["ld","w0"],["qw","e1",512,1024],["ld","w1"],["product1",0],["bn",0],["evac",0,0,"a"],["ld","bo"],["pi","e2",512,768],["bn",1],["evac",0,1,"a"],["ld","x0-4"],["pi","e2",768,1024],["agg",0],["pe","e2","S",512,768,512,1024],["ld","y4-8"],["tr_a"],["rg","e2","V",0,512],["pe","e2","S",768,1024,512,1024],["ld","x4-8"],["pi","e3",512,768],["agg",1],["evac",0,0,"l"],["scales",0,2],["ld","y8-12"],["pi","e3",768,1024],["qw","e2",0,512],["evac",0,1,"l"],["xb",0],["ld","y12-16"],["qw","e2",512,1024],["pe","e3","S",512,768,512,1024],["xb",1],["ld","x8-12"],["rg","e3","V",0,512],["pe","e3","S",768,1024,512,1024],["ld","x12-16"],["qw","e3",0,512],["z",0],["qw","e3",512,1024],["product1",1],["mul",0],["evac",1,0,"s"],["rg","w0","V",0,512],["evac",1,1,"s"],["tr_c"],["qw","w0",0,512],["copy_c"],["pi","w0",512,768],["pe","w0","S",512,768,512,1024],["pi","w0",768,1024],["pe","w0","S",768,1024,512,1024],["pi","w1",512,768],["qw","w0",512,1024],["z",1],["pi","w1",768,1024],["bn",2],["pe","w1","S",512,768,512,1024],["tr",0],["mul",1],["pe","w1","S",768,1024,512,1024],["rg","w1","V",0,512],["sbn",3],["qw","w1",0,512],["silu",0],["tr",1],["qw","w1",512,1024],["agg",2],["scales",2,4],["bn",4],["z",2],["xb",2],["agg",4],["sbn",5],["xb",3],["q",0],["silu",1],["scales",4,6],["mx",0],["mul",2],["z",3],["xb",4],["tr",2],["bn",6],["sbn",7],["q",1],["fin",0],["silu",2],["mx",1],["mul",3],["z",4],["tr",3],["agg",6],["scales",6,8],["bn",8],["xb",5],["q",2],["xb",6],["fin",1],["silu",3],["mx",2],["mul",4],["z",5],["tr",4],["agg",8],["sbn",10],["bn",9],["q",3],["fin",2],["silu",4],["mx",3],["mul",5],["z",6],["tr",5],["agg",9],["scales",8,10],["bn",11],["xb",7],["q",4],["xb",8],["fin",3],["silu",5],["mx",4],["mul",6],["z",7],["tr",6],["agg",11],["sbn",13],["scales",10,12],["bn",12],["xb",9],["q",5],["fin",4],["silu",6],["mx",5],["mul",7],["z",8],["tr",7],["agg",12],["scales",12,14],["bn",14],["xb",10],["q",6],["fin",5],["silu",7],["xb",11],["mx",6],["mul",8],["z",9],["tr",8],["agg",14],["q",7],["fin",6],["silu",8],["mx",7],["mul",9],["z",10],["tr",9],["q",8],["sbn",15],["scales",14,16],["fin",7],["silu",9],["xb",12],["mx",8],["mul",10],["z",11],["xb",13],["tr",10],["q",9],["fin",8],["silu",10],["xb",14],["mx",9],["mul",11],["z",12],["tr",11],["q",10],["fin",9],["silu",11],["xb",15],["mx",10],["mul",12],["z",13],["tr",12],["q",11],["fin",10],["silu",12],["mx",11],["mul",13],["z",14],["tr",13],["q",12],["fin",11],["silu",13],["mx",12],["mul",14],["z",15],["tr",14],["q",13],["fin",12],["silu",14],["mx",13],["mul",15],["tr",15],["q",14],["fin",13],["silu",15],["mx",14],["q",15],["fin",14],["mx",15],["fin",15]],"zb":4,"rb":4,"wg":2,"gg":1,"pre":[0,1,2,3,4,5,6,7,8,9,10,11,12,13,14,15],"mb":3,"pb":6,"vx":[],"xp":4}
 def tile_temporalcrossattention_pa_kernel(tc, x, y, emb0, We, be, ln2_g, ln2_b, Wo, bo, out):
     nc = tc.nc
     with ExitStack() as ctx:
         keep = ctx.enter_context(tc.tile_pool(name="keep", bufs=1))
         we_raw_pool = ctx.enter_context(tc.tile_pool(name="we_raw", bufs=2 * PASSES))
         wo_raw_pool = ctx.enter_context(tc.tile_pool(name="wo_raw", bufs=PASSES))
-        w_grouped_pool = ctx.enter_context(tc.tile_pool(name="w_grouped", bufs=2))
-        z_pool = ctx.enter_context(tc.tile_pool(name="z", bufs=3))
+        w_grouped_pool = ctx.enter_context(tc.tile_pool(name="w_grouped", bufs=CFG["wg"]))
+        gp_grouped_pool = ctx.enter_context(tc.tile_pool(name="gp_grouped", bufs=CFG["gg"]))
+        z_pool = ctx.enter_context(tc.tile_pool(name="z", bufs=CFG["zb"]))
         act_pool = ctx.enter_context(tc.tile_pool(name="act", bufs=3))
-        res_pool = ctx.enter_context(tc.tile_pool(name="res", bufs=5))
+        res_pool = ctx.enter_context(tc.tile_pool(name="res", bufs=CFG["rb"]))
+        mix_pool = ctx.enter_context(tc.tile_pool(name="mix", bufs=CFG["mb"]))
+        pre_pool = ctx.enter_context(tc.tile_pool(name="pre", bufs=CFG["pb"]))
         small = ctx.enter_context(tc.tile_pool(name="small", bufs=4))
         psum_keep = ctx.enter_context(tc.psum_pool(name="psum_keep", bufs=HALVES))
         psum_t = ctx.enter_context(tc.psum_pool(name="psum_t", bufs=3))
         psum_mm = ctx.enter_context(tc.psum_pool(name="psum_mm", bufs=3))
         ctx.enter_context(tc.manual_schedule())
 
-        ident = keep.tile([P, P], F32)
-        make_identity(nc, ident[:])
-        minus_half = keep.tile([P, LOAD_TILES], F32)
-        nc.gpsimd.memset(minus_half[:], -0.5)
         vec_rows = keep.tile([P, P], BF16)
         nc.vector.memset(vec_rows[:].bitcast(I32), 0)
+        ident = keep.tile([P, P], F32)
+        make_identity(nc, ident[:])
+        ident_bf = keep.tile([P, P], BF16)
+        nc.vector.tensor_copy(out=ident_bf[:], in_=ident[:])
+        minus_half = keep.tile([P, LOAD_TILES], F32)
+        nc.gpsimd.memset(minus_half[:], -0.5)
 
         def load_tiles(src, c, name):
             part = keep.tile([P, LOAD_TILES, D], BF16, name=name % c)
@@ -118,109 +122,173 @@ def tile_temporalcrossattention_pa_kernel(tc, x, y, emb0, We, be, ln2_g, ln2_b, 
             return part
 
         emb_raw = keep.tile([P, D], BF16)
-        nc.sync.dma_start(out=emb_raw[:], in_=emb0)
-        nc.sync.dma_start(out=vec_rows[0:16, :], in_=be.rearrange("(r c) -> r c", c=P))
-        nc.sync.dma_start(out=vec_rows[16:24, :], in_=ln2_g.rearrange("(r c) -> r c", c=P))
-        nc.sync.dma_start(out=vec_rows[24:32, :], in_=ln2_b.rearrange("(r c) -> r c", c=P))
-        y_sb = []
-        we_raw = []
-        for side in range(2):
-            y_sb.append(load_tiles(y, side, "y%d"))
-            for g in range(PASSES):
-                we_raw.append(
-                    load_weight_piece(
-                        nc, we_raw_pool,
-                        We[g * K_PASS : (g + 1) * K_PASS, side * W_COLS : (side + 1) * W_COLS],
-                    )
-                )
-        for c in range(2, T // LOAD_TILES):
-            y_sb.append(load_tiles(y, c, "y%d"))
-        wo_raw = [
-            load_weight_piece(nc, wo_raw_pool, Wo[g * K_PASS : (g + 1) * K_PASS, :])
-            for g in range(PASSES)
-        ]
+        y_sb = {}
+        x_sb = {}
+        we_raw = {}
+        wo_raw = {}
         bo_rows = keep.tile([P, D], BF16)
-        nc.sync.dma_start(out=bo_rows[:], in_=bo.partition_broadcast(P))
-        x_sb = [load_tiles(x, c, "x%d") for c in range(T // LOAD_TILES)]
+        def ld(item):
+            if item == "emb":
+                nc.sync.dma_start(out=emb_raw[:], in_=emb0)
+            elif item == "vec":
+                nc.sync.dma_start(out=vec_rows[0:16, :], in_=be.rearrange("(r c) -> r c", c=P))
+                nc.sync.dma_start(out=vec_rows[16:24, :], in_=ln2_g.rearrange("(r c) -> r c", c=P))
+                nc.sync.dma_start(out=vec_rows[24:32, :], in_=ln2_b.rearrange("(r c) -> r c", c=P))
+            elif item == "bo":
+                nc.sync.dma_start(out=bo_rows[:], in_=bo.partition_broadcast(P))
+            elif item[0] in "xy":
+                lo, hi = [int(v) for v in item[1:].split("-")]
+                if item[0] == "x":
+                    part = we_raw_pool.tile([P, PACK, W_COLS], BF16, tag="raw", name="x_" + str(lo))
+                else:
+                    part = keep.tile([P, hi - lo, D], BF16, name=item[0] + "_" + str(lo))
+                nc.sync.dma_start(out=part[:], in_=(y if item[0] == "y" else x)[:, lo:hi, :])
+                for t in range(lo, hi):
+                    (y_sb if item[0] == "y" else x_sb)[t] = part[:, t - lo, :]
+            elif item[0] == "e":
+                c = int(item[1])
+                side, g = divmod(c, PASSES)
+                we_raw[c] = load_weight_piece(
+                    nc, we_raw_pool,
+                    We[g * K_PASS : (g + 1) * K_PASS, side * W_COLS : (side + 1) * W_COLS],
+                )
+            else:
+                g = int(item[1])
+                wo_raw[g] = load_weight_piece(nc, wo_raw_pool, Wo[g * K_PASS : (g + 1) * K_PASS, :])
 
-        emb_f32 = z_pool.tile([P, D], F32, tag="z", name="emb_f32")
-        nc.vector.tensor_copy(out=emb_f32[:], in_=emb_raw[:])
         emb_codes = keep.tile([P, PASSES, P], U32, align_bytes=64)
         emb_scales = keep.tile([P, PASSES, P], U8, align_bytes=64)
-        emb_grouped = silu_out_of_psum(nc, act_pool, transpose_rows(nc, psum_t, emb_f32, None, ident))
-        quantise(
-            nc,
-            emb_grouped[:].rearrange("p g r j -> p (g r j)"),
-            emb_codes[:].rearrange("p g r -> p (g r)"),
-            emb_scales[:].rearrange("p g r -> p (g r)"),
-        )
-
         vec_f32 = keep.tile([P, P], F32)
-        nc.vector.tensor_copy(out=vec_f32[:], in_=vec_rows[:])
-        vec_bank = psum_t.tile([P, PACK, P], F32, tag="kT", name="vec_bank")
-        nc.tensor.transpose(out=vec_bank[:, 0, :], in_=vec_f32[:], identity=ident[:])
         vec_cols = keep.tile([P, 4 * CHUNKS], F32)
-        nc.vector.tensor_copy(out=vec_cols[:], in_=vec_bank[:, 0, 0 : 4 * CHUNKS])
         be_scale = vec_cols[:, 0:CHUNKS]
         be_shift = vec_cols[:, CHUNKS : 2 * CHUNKS]
         gain = vec_cols[:, 2 * CHUNKS : 3 * CHUNKS]
         beta = vec_cols[:, 3 * CHUNKS : 4 * CHUNKS]
         a_bias = keep.tile([P, CHUNKS], F32)
-        nc.vector.scalar_tensor_tensor(
-            out=a_bias[:], in0=be_scale, scalar=1.0, in1=gain, op0=ALU.add, op1=ALU.mult
-        )
         c_bias = keep.tile([P, CHUNKS], F32)
-        nc.vector.scalar_tensor_tensor(
-            out=c_bias[:], in0=be_scale, scalar=1.0, in1=beta, op0=ALU.add, op1=ALU.mult
-        )
-        nc.vector.tensor_tensor(out=c_bias[:], in0=c_bias[:], in1=be_shift, op=ALU.add)
-
         mean_var = keep.tile([P, T, 2], F32)
         rstd = keep.tile([P, T], F32)
         z_bias = keep.tile([P, T], F32)
-
-        def row_moments(c):
-            for i in range(LOAD_TILES):
-                stats = small.tile([P, D // BN_MAX, BN_DIM], F32, name="stats")
-                for s in range(D // BN_MAX):
-                    nc.vector.bn_stats(
-                        out=stats[:, s, :], in_=y_sb[c][:, i, s * BN_MAX : (s + 1) * BN_MAX]
-                    )
-                nc.vector.bn_aggr(
-                    out=mean_var[:, c * LOAD_TILES + i, :], in_=stats[:].rearrange("p s k -> p (s k)")
-                )
-
-        def row_scales(c):
-            tiles = slice(c * LOAD_TILES, (c + 1) * LOAD_TILES)
-            var_eps = small.tile([P, LOAD_TILES], F32, name="var_eps")
-            nc.gpsimd.tensor_scalar(
-                out=var_eps[:], in0=mean_var[:, tiles, 1], scalar1=1.0, scalar2=EPS,
-                op0=ALU.mult, op1=ALU.add,
-            )
-            nc.gpsimd.tensor_tensor(out=rstd[:, tiles], in0=var_eps[:], in1=minus_half[:], op=ALU.pow)
-            neg_mean = small.tile([P, LOAD_TILES], F32, name="neg_mean")
-            nc.gpsimd.tensor_scalar(
-                out=neg_mean[:], in0=mean_var[:, tiles, 0], scalar1=-1.0, scalar2=0.0,
-                op0=ALU.mult, op1=ALU.add,
-            )
-            nc.gpsimd.tensor_tensor(out=z_bias[:, tiles], in0=neg_mean[:], in1=rstd[:, tiles], op=ALU.mult)
-
         we_codes = keep.tile([P, 2 * PASSES, W_COLS], U32, align_bytes=64)
         we_scales = keep.tile([P, 2 * PASSES, W_COLS], U8, align_bytes=64)
-        for side in range(2):
-            row_moments(side)
-            for g in range(PASSES):
-                c = side * PASSES + g
-                we_grouped = regroup_weight_piece(nc, w_grouped_pool, we_raw[c])
-                quantise(
-                    nc, we_grouped[:].rearrange("p n j -> p (n j)"), we_codes[:, c, :], we_scales[:, c, :]
-                )
-            row_scales(side)
-
+        wo_codes = keep.tile([P, PASSES, W_COLS], U32, align_bytes=64)
+        wo_scales = keep.tile([P, PASSES, W_COLS], U8, align_bytes=64)
         a_t = res_pool.tile([P, D], F32, tag="res", name="a_t")
         l_t = res_pool.tile([P, D], F32, tag="res", name="l_t")
         s_t = res_pool.tile([P, D], F32, tag="res", name="s_t")
-        for side in range(2):
+        c_rows = keep.tile([P, D], F32)
+        st = {"stats": {}}
+        grouped = {}
+        e_banks = {}
+
+        def tr_e():
+            st["e"] = transpose_rows(nc, psum_t, emb_raw, None, ident_bf)
+
+        def silu_e():
+            st["eg"] = silu_out_of_psum(nc, act_pool, st["e"])
+
+        def q_e():
+            quantise(
+                nc,
+                st["eg"][:].rearrange("p g r j -> p (g r j)"),
+                emb_codes[:].rearrange("p g r -> p (g r)"),
+                emb_scales[:].rearrange("p g r -> p (g r)"),
+            )
+
+        def vec():
+            nc.vector.tensor_copy(out=vec_f32[:], in_=vec_rows[:])
+            vec_bank = psum_mm.tile([P, PACK, P], F32, tag="mm", name="vec_bank")
+            nc.tensor.transpose(out=vec_bank[:, 0, :], in_=vec_f32[:], identity=ident[:])
+            nc.vector.tensor_copy(out=vec_cols[:], in_=vec_bank[:, 0, 0 : 4 * CHUNKS])
+            nc.vector.scalar_tensor_tensor(
+                out=a_bias[:], in0=be_scale, scalar=1.0, in1=gain, op0=ALU.add, op1=ALU.mult
+            )
+            nc.vector.scalar_tensor_tensor(
+                out=c_bias[:], in0=be_scale, scalar=1.0, in1=beta, op0=ALU.add, op1=ALU.mult
+            )
+            nc.vector.tensor_tensor(out=c_bias[:], in0=c_bias[:], in1=be_shift, op=ALU.add)
+
+        def sbn(t):
+            src = y_sb[t]
+            total = small.tile([P, 1], F32, name="total")
+            junk = keep.tile([P, D], BF16, name="junk") if "junk" not in st else st["junk"]
+            st["junk"] = junk
+            nc.scalar.activation(out=junk[:], in_=src, func=ACT.Identity, accum_out=total[:])
+            shift = small.tile([P, 1], F32, name="shift")
+            nc.scalar.mul(shift[:], total[:], 1.0 / (32.0 * D))
+            nc.scalar.mul(mean_var[:, t, 0:1], total[:], 1.0 / D)
+            nc.scalar.activation(
+                out=junk[:], in_=src, func=ACT.Square, scale=-1.0 / 32.0, bias=shift[:],
+                accum_out=mean_var[:, t, 1:2],
+            )
+
+        def bn(t):
+            stats = small.tile([P, D // BN_MAX, BN_DIM], F32, name="stats")
+            for s in range(D // BN_MAX):
+                nc.vector.bn_stats(
+                    out=stats[:, s, :], in_=y_sb[t][:, s * BN_MAX : (s + 1) * BN_MAX]
+                )
+            st["stats"][t] = stats
+
+        def agg(t):
+            nc.vector.bn_aggr(
+                out=mean_var[:, t, :], in_=st["stats"][t][:].rearrange("p s k -> p (s k)")
+            )
+
+        def scales(lo, hi):
+            tiles = slice(lo, hi)
+            var_eps = small.tile([P, LOAD_TILES], F32, name="var_eps")
+            n = hi - lo
+            nc.gpsimd.tensor_scalar(
+                out=var_eps[:, 0:n], in0=mean_var[:, tiles, 1], scalar1=1.0, scalar2=EPS,
+                op0=ALU.mult, op1=ALU.add,
+            )
+            nc.gpsimd.tensor_tensor(out=rstd[:, tiles], in0=var_eps[:, 0:n], in1=minus_half[:, 0:n], op=ALU.pow)
+            neg_mean = small.tile([P, LOAD_TILES], F32, name="neg_mean")
+            nc.gpsimd.tensor_scalar(
+                out=neg_mean[:, 0:n], in0=mean_var[:, tiles, 0], scalar1=-1.0, scalar2=0.0,
+                op0=ALU.mult, op1=ALU.add,
+            )
+            nc.gpsimd.tensor_tensor(out=z_bias[:, tiles], in0=neg_mean[:, 0:n], in1=rstd[:, tiles], op=ALU.mult)
+
+        def rg(name, eng, lo, hi):
+            pool = w_grouped_pool if eng != "G" else gp_grouped_pool
+            grouped[name, lo] = pool.tile([P, hi - lo, PACK], BF16, align_bytes=64, name="wg_" + eng + str(hi - lo))
+            raw = we_raw[int(name[1])] if name[0] == "e" else wo_raw[int(name[1])]
+            regroup(nc, grouped[name, lo], raw, eng, lo, hi)
+
+        def pi(name, lo, hi):
+            raw = we_raw[int(name[1])] if name[0] == "e" else wo_raw[int(name[1])]
+            bank = psum_t.tile([P, hi - lo, PACK], BF16, tag="kT", name="il")
+            for a in range(0, hi - lo, P):
+                nc.tensor.matmul(
+                    out=bank[:, a : a + P, :], lhsT=ident_bf[:],
+                    rhs=raw[:, :, lo + a : lo + a + P].rearrange("p j n -> p n j"), start=True, stop=True,
+                )
+            st["il", name, lo] = bank
+
+        def pe(name, eng, lo, hi, base, top):
+            if (name, base) not in grouped:
+                grouped[name, base] = w_grouped_pool.tile([P, top - base, PACK], BF16, align_bytes=64, name="wp_" + str(top - base))
+            dst = grouped[name, base][:, lo - base : hi - base, :]
+            if eng == "S":
+                nc.scalar.copy(out=dst, in_=st["il", name, lo][:])
+            else:
+                nc.vector.tensor_copy(out=dst, in_=st["il", name, lo][:])
+
+        def qw(name, lo, hi):
+            c = int(name[1])
+            codes, scl = (we_codes, we_scales) if name[0] == "e" else (wo_codes, wo_scales)
+            a = lo
+            for w in (1024, 512, 256, 128):
+                while hi - a >= w:
+                    quantise(
+                        nc, grouped[name, lo][:, a - lo : a - lo + w, :].rearrange("p n j -> p (n j)"),
+                        codes[:, c, a : a + w], scl[:, c, a : a + w],
+                    )
+                    a += w
+
+        def product1(side):
             for h in range(HALVES):
                 e_bank = psum_mm.tile([P, PACK, P], F32, tag="mm", name="e_bank")
                 for i in range(PACK):
@@ -235,41 +303,38 @@ def tile_temporalcrossattention_pa_kernel(tc, x, y, emb0, We, be, ln2_g, ln2_b, 
                             start=(g == 0),
                             stop=(g == PASSES - 1),
                         )
-                for i in range(PACK):
-                    k = h * PACK + i
-                    cols = slice(k * P, (k + 1) * P)
-                    if side == 0:
-                        nc.scalar.activation(
-                            out=a_t[:, cols], in_=e_bank[:, i, :], func=ACT.Identity,
-                            scale=gain[:, k : k + 1], bias=a_bias[:, k : k + 1],
-                        )
-                        nc.scalar.activation(
-                            out=l_t[:, cols], in_=e_bank[:, i, :], func=ACT.Identity,
-                            scale=beta[:, k : k + 1],
-                        )
-                    else:
-                        nc.scalar.activation(
-                            out=s_t[:, cols], in_=e_bank[:, i, :], func=ACT.Identity,
-                            bias=c_bias[:, k : k + 1],
-                        )
-        a_banks = transpose_rows(nc, psum_keep, a_t, None, ident)
-        c_banks = transpose_rows(nc, psum_t, s_t, l_t, ident)
-        c_rows = keep.tile([P, D], F32)
-        for h in range(HALVES):
-            nc.scalar.copy(
-                out=c_rows[:, h * BANK : (h + 1) * BANK], in_=c_banks[h][:].rearrange("p i d -> p (i d)")
-            )
+                e_banks[side, h] = e_bank
 
-        wo_codes = keep.tile([P, PASSES, W_COLS], U32, align_bytes=64)
-        wo_scales = keep.tile([P, PASSES, W_COLS], U8, align_bytes=64)
-        wo_grouped = [regroup_weight_piece(nc, w_grouped_pool, wo_raw[g]) for g in range(PASSES)]
-        for c in range(2, T // LOAD_TILES):
-            row_moments(c)
-            row_scales(c)
-        for g in range(PASSES):
-            quantise(
-                nc, wo_grouped[g][:].rearrange("p n j -> p (n j)"), wo_codes[:, g, :], wo_scales[:, g, :]
-            )
+        def evac(side, h, what):
+            for i in range(PACK):
+                k = h * PACK + i
+                cols = slice(k * P, (k + 1) * P)
+                src = e_banks[side, h][:, i, :]
+                if what == "a":
+                    nc.scalar.activation(
+                        out=a_t[:, cols], in_=src, func=ACT.Identity,
+                        scale=gain[:, k : k + 1], bias=a_bias[:, k : k + 1],
+                    )
+                elif what == "l":
+                    nc.scalar.activation(
+                        out=l_t[:, cols], in_=src, func=ACT.Identity, scale=beta[:, k : k + 1]
+                    )
+                else:
+                    nc.scalar.activation(
+                        out=s_t[:, cols], in_=src, func=ACT.Identity, bias=c_bias[:, k : k + 1]
+                    )
+
+        def tr_a():
+            st["a"] = transpose_rows(nc, psum_keep, a_t, None, ident)
+
+        def tr_c():
+            st["c"] = transpose_rows(nc, psum_t, s_t, l_t, ident)
+
+        def copy_c():
+            for h in range(HALVES):
+                nc.scalar.copy(
+                    out=c_rows[:, h * BANK : (h + 1) * BANK], in_=st["c"][h][:].rearrange("p i d -> p (i d)")
+                )
 
         z_tiles = {}
         h_banks = {}
@@ -279,47 +344,58 @@ def tile_temporalcrossattention_pa_kernel(tc, x, y, emb0, We, be, ln2_g, ln2_b, 
         products = {}
         residual = {}
 
-        def residual_plus_bias(t):
-            res = res_pool.tile([P, D], F32, tag="res", name="res")
-            nc.gpsimd.tensor_tensor(
-                out=res[:], in0=x_sb[t // LOAD_TILES][:, t % LOAD_TILES, :], in1=bo_rows[:], op=ALU.add
-            )
-            residual[t] = res
+        def xb(t):
+            if t in CFG["pre"]:
+                residual[t] = pre_pool.tile([P, D], F32, tag="pre", name="pre")
+            else:
+                residual[t] = mix_pool.tile([P, D], F32, align_bytes=64, tag="mix", name="xbo")
+            w = D // CFG["xp"]
+            if t in CFG["vx"]:
+                for i in range(1):
+                    nc.vector.tensor_tensor(out=residual[t][:], in0=x_sb[t], in1=bo_rows[:], op=ALU.add)
+                return
+            for i in range(CFG["xp"]):
+                cols = slice(i * w, (i + 1) * w)
+                nc.gpsimd.tensor_tensor(
+                    out=residual[t][:, cols], in0=x_sb[t][:, cols], in1=bo_rows[:, cols], op=ALU.add,
+                )
 
-        def normalise(t):
-            z = z_pool.tile([P, D], F32, tag="z", name="z")
+        def z(t):
+            zt = z_pool.tile([P, D], F32, tag="z", name="z")
             nc.scalar.activation(
-                out=z[:], in_=y_sb[t // LOAD_TILES][:, t % LOAD_TILES, :], func=ACT.Identity,
+                out=zt[:], in_=y_sb[t], func=ACT.Identity,
                 scale=rstd[:, t : t + 1], bias=z_bias[:, t : t + 1],
             )
-            z_tiles[t] = z
+            z_tiles[t] = zt
 
-        def modulate_and_transpose(t):
-            z = z_tiles[t]
+        def mul(t):
+            zt = z_tiles[t]
             for h in range(HALVES):
                 cols = slice(h * BANK, (h + 1) * BANK)
                 nc.vector.tensor_tensor(
-                    out=z[:, cols], in0=z[:, cols], in1=a_banks[h][:].rearrange("p i d -> p (i d)"),
+                    out=zt[:, cols], in0=zt[:, cols], in1=st["a"][h][:].rearrange("p i d -> p (i d)"),
                     op=ALU.mult,
                 )
-            h_banks[t] = transpose_rows(nc, psum_t, z, c_rows, ident)
 
-        def activate(t):
-            act_grouped[t] = silu_out_of_psum(nc, act_pool, h_banks[t])
+        def tr(t):
+            h_banks[t] = transpose_rows(nc, psum_t, z_tiles[t], c_rows, ident)
 
-        def quantise_tile(t):
+        def silu(t):
+            act_grouped[t] = silu_out_of_psum(nc, mix_pool, h_banks[t], "mix")
+
+        def q(t):
             codes = act_pool.tile([P, PASSES, P], U32, align_bytes=64, tag="act_codes", name="act_codes")
-            scales = act_pool.tile([P, PASSES, P], U8, align_bytes=64, tag="act_scales", name="act_scales")
+            scl = act_pool.tile([P, PASSES, P], U8, align_bytes=64, tag="act_scales", name="act_scales")
             quantise(
                 nc,
                 act_grouped[t][:].rearrange("p g r j -> p (g r j)"),
                 codes[:].rearrange("p g r -> p (g r)"),
-                scales[:].rearrange("p g r -> p (g r)"),
+                scl[:].rearrange("p g r -> p (g r)"),
             )
             act_codes[t] = codes
-            act_scales[t] = scales
+            act_scales[t] = scl
 
-        def project(t):
+        def mx(t):
             products[t] = []
             for h in range(HALVES):
                 cols = slice(h * BANK, (h + 1) * BANK)
@@ -336,26 +412,15 @@ def tile_temporalcrossattention_pa_kernel(tc, x, y, emb0, We, be, ln2_g, ln2_b, 
                     )
                 products[t].append(acc)
 
-        def finish(t):
-            res = residual[t]
+        def fin(t):
+            res = res_pool.tile([P, D], F32, tag="res", name="res")
             for h in range(HALVES):
                 cols = slice(h * BANK, (h + 1) * BANK)
-                nc.vector.tensor_tensor(out=res[:, cols], in0=products[t][h][:], in1=res[:, cols], op=ALU.add)
+                nc.vector.tensor_tensor(out=res[:, cols], in0=products[t][h][:], in1=residual[t][:, cols], op=ALU.add)
             nc.sync.dma_start(out=out[:, t, :], in_=res[:])
 
-        normalise(0)
-        for i in range(T + 2):
-            if i < T:
-                residual_plus_bias(i)
-            if 1 <= i <= T:
-                activate(i - 1)
-            if i + 1 < T:
-                normalise(i + 1)
-            if i < T:
-                modulate_and_transpose(i)
-            if 1 <= i <= T:
-                quantise_tile(i - 1)
-            if i >= 2:
-                finish(i - 2)
-            if 1 <= i <= T:
-                project(i - 1)
+        names = {"ld": ld, "pi": pi, "pe": pe, "sbn": sbn, "tr_e": tr_e, "silu_e": silu_e, "q_e": q_e, "vec": vec, "bn": bn, "agg": agg, "scales": scales, "rg": rg, "qw": qw,
+                 "product1": product1, "evac": evac, "tr_a": tr_a, "tr_c": tr_c, "copy_c": copy_c,
+                 "xb": xb, "z": z, "mul": mul, "tr": tr, "silu": silu, "q": q, "mx": mx, "fin": fin}
+        for op in CFG["ops"]:
+            names[op[0]](*op[1:])

@@ -39,7 +39,7 @@ def load_weight_piece(nc, pool, rows):
 def regroup(nc, grouped, raw, engine, lo, hi):
     if engine == "G":
         nc.gpsimd.tensor_scalar(
-            out=grouped[:],
+            out=grouped,
             in0=raw[:, :, lo:hi].rearrange("p j n -> p n j"),
             scalar1=1.0,
             scalar2=0.0,
@@ -49,7 +49,7 @@ def regroup(nc, grouped, raw, engine, lo, hi):
     else:
         copy = nc.scalar.copy if engine == "S" else nc.vector.tensor_copy
         copy(
-            out=grouped[:].rearrange("p (c i) j -> p c j i", i=4),
+            out=grouped.rearrange("p (c i) j -> p c j i", i=4),
             in_=raw[:, :, lo:hi].rearrange("p j (c i) -> p c j i", i=4),
         )
 
@@ -87,7 +87,7 @@ def silu_out_of_psum(nc, pool, banks, tag="act_grouped"):
     return grouped
 
 
-CFG = {"dma":["emb","e0","vec","e1","y0-2","e2","e3","y2-4","w0","w1","bo","x0-4","y4-8","x4-8","y8-12","y12-16","x8-12","x12-16"],"ops":[["ld","emb"],["tr_e"],["silu_e"],["ld","e0"],["pi","e0",512,768],["q_e"],["pe","e0","S",512,768,512,1024],["ld","vec"],["pi","e0",768,1024],["vec"],["pe","e0","S",768,1024,512,1024],["ld","e1"],["pi","e1",512,768],["rg","e0","V",0,512],["pe","e1","S",512,768,512,1024],["ld","y0-2"],["pi","e1",768,1024],["qw","e0",0,512],["pe","e1","S",768,1024,512,1024],["ld","e2"],["qw","e0",512,1024],["ld","e3"],["rg","e1","V",0,512],["ld","y2-4"],["qw","e1",0,512],["ld","w0"],["qw","e1",512,1024],["ld","w1"],["product1",0],["bn",0],["evac",0,0,"a"],["ld","bo"],["pi","e2",512,768],["bn",1],["evac",0,1,"a"],["ld","x0-4"],["pi","e2",768,1024],["agg",0],["pe","e2","S",512,768,512,1024],["ld","y4-8"],["tr_a"],["rg","e2","V",0,512],["pe","e2","S",768,1024,512,1024],["ld","x4-8"],["pi","e3",512,768],["agg",1],["evac",0,0,"l"],["scales",0,2],["ld","y8-12"],["pi","e3",768,1024],["qw","e2",0,512],["evac",0,1,"l"],["xb",0],["ld","y12-16"],["qw","e2",512,1024],["pe","e3","S",512,768,512,1024],["xb",1],["ld","x8-12"],["rg","e3","V",0,512],["pe","e3","S",768,1024,512,1024],["ld","x12-16"],["qw","e3",0,512],["z",0],["qw","e3",512,1024],["product1",1],["mul",0],["evac",1,0,"s"],["rg","w0","V",0,512],["evac",1,1,"s"],["tr_c"],["qw","w0",0,512],["copy_c"],["pi","w0",512,768],["pe","w0","S",512,768,512,1024],["pi","w0",768,1024],["pe","w0","S",768,1024,512,1024],["pi","w1",512,768],["qw","w0",512,1024],["z",1],["pi","w1",768,1024],["bn",2],["pe","w1","S",512,768,512,1024],["tr",0],["mul",1],["pe","w1","S",768,1024,512,1024],["rg","w1","V",0,512],["sbn",3],["qw","w1",0,512],["silu",0],["tr",1],["qw","w1",512,1024],["agg",2],["scales",2,4],["bn",4],["z",2],["xb",2],["agg",4],["sbn",5],["xb",3],["q",0],["silu",1],["scales",4,6],["mx",0],["mul",2],["z",3],["xb",4],["tr",2],["bn",6],["sbn",7],["q",1],["fin",0],["silu",2],["mx",1],["mul",3],["z",4],["tr",3],["agg",6],["scales",6,8],["bn",8],["xb",5],["q",2],["xb",6],["fin",1],["silu",3],["mx",2],["mul",4],["z",5],["tr",4],["agg",8],["sbn",10],["bn",9],["q",3],["fin",2],["silu",4],["mx",3],["mul",5],["z",6],["tr",5],["agg",9],["scales",8,10],["bn",11],["xb",7],["q",4],["xb",8],["fin",3],["silu",5],["mx",4],["mul",6],["z",7],["tr",6],["agg",11],["sbn",13],["scales",10,12],["bn",12],["xb",9],["q",5],["fin",4],["silu",6],["mx",5],["mul",7],["z",8],["tr",7],["agg",12],["scales",12,14],["bn",14],["xb",10],["q",6],["fin",5],["silu",7],["xb",11],["mx",6],["mul",8],["z",9],["tr",8],["agg",14],["q",7],["fin",6],["silu",8],["mx",7],["mul",9],["z",10],["tr",9],["q",8],["sbn",15],["scales",14,16],["fin",7],["silu",9],["xb",12],["mx",8],["mul",10],["z",11],["xb",13],["tr",10],["q",9],["fin",8],["silu",10],["xb",14],["mx",9],["mul",11],["z",12],["tr",11],["q",10],["fin",9],["silu",11],["xb",15],["mx",10],["mul",12],["z",13],["tr",12],["q",11],["fin",10],["silu",12],["mx",11],["mul",13],["z",14],["tr",13],["q",12],["fin",11],["silu",13],["mx",12],["mul",14],["z",15],["tr",14],["q",13],["fin",12],["silu",14],["mx",13],["mul",15],["tr",15],["q",14],["fin",13],["silu",15],["mx",14],["q",15],["fin",14],["mx",15],["fin",15]],"zb":4,"rb":4,"wg":2,"gg":1,"pre":[0,1,2,3,4,5,6,7,8,9,10,11,12,13,14,15],"mb":3,"pb":6,"vx":[],"xp":4}
+CFG = {"dma":["y0-1","emb","y1-2","vec","y2-4","e0","y4-6","e1","e2","y6-8","e3","w0","y8-12","w1","bo","x0-4","y12-16","x4-8","x8-12","x12-16"],"ops":[["ld","y0-1"],["bn",0],["ld","emb"],["tr_e"],["silu_e"],["ld","y1-2"],["q_e"],["ld","vec"],["vec_t"],["vec_a"],["ld","y2-4"],["bn",1],["ld","e0"],["vec_b"],["rg","e0","S",0,640],["rg","e0","G",640,768],["ld","y4-6"],["agg",0],["rg","e0","G",768,896],["ld","e1"],["bn",2],["rg","e1","S",0,640],["rg","e0","G",896,1024],["ld","e2"],["vec"],["rg","e2","S",0,640],["rg","e1","G",640,768],["ld","y6-8"],["agg",1],["rg","e1","G",768,896],["ld","e3"],["bn",3],["rg","e1","G",896,1024],["ld","w0"],["agg",2],["rg","e2","G",640,768],["ld","y8-12"],["bn",4],["rg","e2","G",768,896],["ld","w1"],["agg",3],["sv",0,4],["rg","e2","G",896,1024],["ld","bo"],["qw","e0"],["scales",0,4],["ld","x0-4"],["agg",4],["rg","e3","G",640,768],["ld","y12-16"],["bn",5],["rg","e3","G",768,896],["ld","x4-8"],["bn",6],["rg","e3","G",896,1024],["ld","x8-12"],["agg",5],["qw","e1"],["product1",0],["agg",6],["evac",0,0,"a"],["bn",7],["evac",0,1,"a"],["tr_a"],["bn",8],["rg","e3","S",0,640],["ld","x12-16"],["agg",7],["sv",4,8],["scales",4,8],["qw","e2"],["z",0],["rg","w0","G",512,640],["agg",8],["evac",0,0,"l"],["rg","w0","G",640,768],["bn",9],["evac",0,1,"l"],["rg","w0","G",768,896],["bn",10],["rg","w0","S",0,512],["rg","w0","G",896,1024],["agg",9],["z",1],["rg","w1","G",512,640],["mul",0],["rg","w1","G",640,768],["agg",10],["rg","w1","G",768,896],["qw","e3"],["rg","w1","G",896,1024],["product1",1],["bn",11],["evac",1,0,"s"],["xb",0],["mul",1],["evac",1,1,"s"],["tr_c"],["agg",11],["copy_c"],["tr",0],["qw","w0"],["rg","w1","S",0,512],["bn",12],["sv",8,12],["scales",8,12],["agg",12],["silu",0],["xb",1],["tr",1],["qw","w1"],["silu",1],["xb",2],["q",0],["z",2],["xb",3],["mx",0],["mul",2],["z",3],["xb",4],["tr",2],["mul",3],["z",4],["xb",5],["fin",0],["z",5],["xb",6],["mul",4],["silu",2],["tr",3],["sbn",13],["mx",1],["fin",1],["silu",3],["xb",7],["tr",4],["bn",14],["z",6],["agg",14],["z",7],["mul",5],["silu",4],["tr",5],["q",1],["sbn",15],["mx",2],["mul",6],["sv",12,16],["scales",12,16],["mul",7],["silu",5],["fin",2],["z",8],["xb",8],["mx",3],["q",2],["z",9],["tr",6],["fin",3],["silu",6],["xb",9],["tr",7],["mul",8],["silu",7],["mx",4],["mul",9],["z",10],["fin",4],["z",11],["xb",10],["mx",5],["q",3],["tr",8],["fin",5],["silu",8],["xb",11],["tr",9],["mul",10],["silu",9],["mx",6],["mul",11],["z",12],["fin",6],["z",13],["xb",12],["mx",7],["q",4],["tr",10],["fin",7],["silu",10],["xb",13],["tr",11],["mul",12],["silu",11],["mx",8],["mul",13],["z",14],["fin",8],["z",15],["xb",14],["mx",9],["q",5],["tr",12],["fin",9],["silu",12],["xb",15],["tr",13],["mul",14],["silu",13],["mx",10],["mul",15],["fin",10],["mx",11],["q",6],["tr",14],["fin",11],["silu",14],["tr",15],["silu",15],["mx",12],["fin",12],["mx",13],["q",7],["fin",13],["mx",14],["fin",14],["mx",15],["fin",15]],"zb":6,"rb":4,"wg":3,"gg":1,"pre":[0,1,2,3,4,5,6,7,8,9,10,11,12,13,14,15],"pb":6,"mb":3,"xp":1,"vx":[],"whole":True,"pair":True}
 def tile_temporalcrossattention_pa_kernel(tc, x, y, emb0, We, be, ln2_g, ln2_b, Wo, bo, out):
     nc = tc.nc
     with ExitStack() as ctx:
@@ -158,7 +158,6 @@ def tile_temporalcrossattention_pa_kernel(tc, x, y, emb0, We, be, ln2_g, ln2_b, 
 
         emb_codes = keep.tile([P, PASSES, P], U32, align_bytes=64)
         emb_scales = keep.tile([P, PASSES, P], U8, align_bytes=64)
-        vec_f32 = keep.tile([P, P], F32)
         vec_cols = keep.tile([P, 4 * CHUNKS], F32)
         be_scale = vec_cols[:, 0:CHUNKS]
         be_shift = vec_cols[:, CHUNKS : 2 * CHUNKS]
@@ -169,6 +168,11 @@ def tile_temporalcrossattention_pa_kernel(tc, x, y, emb0, We, be, ln2_g, ln2_b, 
         mean_var = keep.tile([P, T, 2], F32)
         rstd = keep.tile([P, T], F32)
         z_bias = keep.tile([P, T], F32)
+        var_eps = keep.tile([P, T], F32)
+        neg_mean = keep.tile([P, T], F32)
+        eps_col = keep.tile([P, 1], F32)
+        nc.gpsimd.memset(eps_col[:], 0.0)
+        nc.gpsimd.tensor_scalar(out=eps_col[:], in0=eps_col[:], scalar1=1.0, scalar2=EPS, op0=ALU.mult, op1=ALU.add)
         we_codes = keep.tile([P, 2 * PASSES, W_COLS], U32, align_bytes=64)
         we_scales = keep.tile([P, 2 * PASSES, W_COLS], U8, align_bytes=64)
         wo_codes = keep.tile([P, PASSES, W_COLS], U32, align_bytes=64)
@@ -195,17 +199,23 @@ def tile_temporalcrossattention_pa_kernel(tc, x, y, emb0, We, be, ln2_g, ln2_b, 
                 emb_scales[:].rearrange("p g r -> p (g r)"),
             )
 
-        def vec():
-            nc.vector.tensor_copy(out=vec_f32[:], in_=vec_rows[:])
-            vec_bank = psum_mm.tile([P, PACK, P], F32, tag="mm", name="vec_bank")
-            nc.tensor.transpose(out=vec_bank[:, 0, :], in_=vec_f32[:], identity=ident[:])
-            nc.vector.tensor_copy(out=vec_cols[:], in_=vec_bank[:, 0, 0 : 4 * CHUNKS])
+        def vec_t():
+            bank = psum_mm.tile([P, PACK, P], BF16, tag="mm", name="vec_bank")
+            nc.tensor.transpose(out=bank[:, 0, :], in_=vec_rows[:], identity=ident_bf[:])
+            st["vec"] = bank
+
+        def vec_a():
+            nc.vector.tensor_copy(out=vec_cols[:], in_=st["vec"][:, 0, 0 : 4 * CHUNKS])
+
+        def vec_b():
             nc.vector.scalar_tensor_tensor(
                 out=a_bias[:], in0=be_scale, scalar=1.0, in1=gain, op0=ALU.add, op1=ALU.mult
             )
             nc.vector.scalar_tensor_tensor(
                 out=c_bias[:], in0=be_scale, scalar=1.0, in1=beta, op0=ALU.add, op1=ALU.mult
             )
+
+        def vec():
             nc.vector.tensor_tensor(out=c_bias[:], in0=c_bias[:], in1=be_shift, op=ALU.add)
 
         def sbn(t):
@@ -235,27 +245,18 @@ def tile_temporalcrossattention_pa_kernel(tc, x, y, emb0, We, be, ln2_g, ln2_b, 
                 out=mean_var[:, t, :], in_=st["stats"][t][:].rearrange("p s k -> p (s k)")
             )
 
+        def sv(lo, hi):
+            nc.scalar.activation(out=var_eps[:, lo:hi], in_=mean_var[:, lo:hi, 1], func=ACT.Identity, bias=eps_col[:])
+            nc.scalar.mul(neg_mean[:, lo:hi], mean_var[:, lo:hi, 0], -1.0)
+
         def scales(lo, hi):
-            tiles = slice(lo, hi)
-            var_eps = small.tile([P, LOAD_TILES], F32, name="var_eps")
-            n = hi - lo
-            nc.gpsimd.tensor_scalar(
-                out=var_eps[:, 0:n], in0=mean_var[:, tiles, 1], scalar1=1.0, scalar2=EPS,
-                op0=ALU.mult, op1=ALU.add,
-            )
-            nc.gpsimd.tensor_tensor(out=rstd[:, tiles], in0=var_eps[:, 0:n], in1=minus_half[:, 0:n], op=ALU.pow)
-            neg_mean = small.tile([P, LOAD_TILES], F32, name="neg_mean")
-            nc.gpsimd.tensor_scalar(
-                out=neg_mean[:, 0:n], in0=mean_var[:, tiles, 0], scalar1=-1.0, scalar2=0.0,
-                op0=ALU.mult, op1=ALU.add,
-            )
-            nc.gpsimd.tensor_tensor(out=z_bias[:, tiles], in0=neg_mean[:, 0:n], in1=rstd[:, tiles], op=ALU.mult)
+            nc.gpsimd.tensor_tensor(out=rstd[:, lo:hi], in0=var_eps[:, lo:hi], in1=minus_half[:, 0 : hi - lo], op=ALU.pow)
 
         def rg(name, eng, lo, hi):
-            pool = w_grouped_pool if eng != "G" else gp_grouped_pool
-            grouped[name, lo] = pool.tile([P, hi - lo, PACK], BF16, align_bytes=64, name="wg_" + eng + str(hi - lo))
+            if name not in grouped:
+                grouped[name] = w_grouped_pool.tile([P, W_COLS, PACK], BF16, align_bytes=64, name="grouped")
             raw = we_raw[int(name[1])] if name[0] == "e" else wo_raw[int(name[1])]
-            regroup(nc, grouped[name, lo], raw, eng, lo, hi)
+            regroup(nc, grouped[name][:, lo:hi, :], raw, eng, lo, hi)
 
         def pi(name, lo, hi):
             raw = we_raw[int(name[1])] if name[0] == "e" else wo_raw[int(name[1])]
@@ -276,17 +277,10 @@ def tile_temporalcrossattention_pa_kernel(tc, x, y, emb0, We, be, ln2_g, ln2_b, 
             else:
                 nc.vector.tensor_copy(out=dst, in_=st["il", name, lo][:])
 
-        def qw(name, lo, hi):
+        def qw(name):
             c = int(name[1])
             codes, scl = (we_codes, we_scales) if name[0] == "e" else (wo_codes, wo_scales)
-            a = lo
-            for w in (1024, 512, 256, 128):
-                while hi - a >= w:
-                    quantise(
-                        nc, grouped[name, lo][:, a - lo : a - lo + w, :].rearrange("p n j -> p (n j)"),
-                        codes[:, c, a : a + w], scl[:, c, a : a + w],
-                    )
-                    a += w
+            quantise(nc, grouped[name][:].rearrange("p n j -> p (n j)"), codes[:, c, :], scl[:, c, :])
 
         def product1(side):
             for h in range(HALVES):
@@ -361,6 +355,9 @@ def tile_temporalcrossattention_pa_kernel(tc, x, y, emb0, We, be, ln2_g, ln2_b, 
                 )
 
         def z(t):
+            nc.scalar.activation(
+                out=z_bias[:, t : t + 1], in_=neg_mean[:, t : t + 1], func=ACT.Identity, scale=rstd[:, t : t + 1]
+            )
             zt = z_pool.tile([P, D], F32, tag="z", name="z")
             nc.scalar.activation(
                 out=zt[:], in_=y_sb[t], func=ACT.Identity,
@@ -381,19 +378,25 @@ def tile_temporalcrossattention_pa_kernel(tc, x, y, emb0, We, be, ln2_g, ln2_b, 
             h_banks[t] = transpose_rows(nc, psum_t, z_tiles[t], c_rows, ident)
 
         def silu(t):
-            act_grouped[t] = silu_out_of_psum(nc, mix_pool, h_banks[t], "mix")
+            j, i = divmod(t, 2)
+            if i == 0:
+                act_grouped[j] = act_pool.tile([P, 2, PASSES, P, PACK], BF16, align_bytes=64, tag="act_pair", name="act_pair")
+            for g in range(PASSES):
+                nc.scalar.activation(
+                    out=act_grouped[j][:, i, g, :, :], in_=h_banks[t][g][:].rearrange("p j r -> p r j"), func=ACT.Silu
+                )
 
-        def q(t):
-            codes = act_pool.tile([P, PASSES, P], U32, align_bytes=64, tag="act_codes", name="act_codes")
-            scl = act_pool.tile([P, PASSES, P], U8, align_bytes=64, tag="act_scales", name="act_scales")
+        def q(j):
+            codes = act_pool.tile([P, 2, PASSES, P], U32, align_bytes=64, tag="act_codes", name="act_codes")
+            scl = act_pool.tile([P, 2, PASSES, P], U8, align_bytes=64, tag="act_scales", name="act_scales")
             quantise(
                 nc,
-                act_grouped[t][:].rearrange("p g r j -> p (g r j)"),
-                codes[:].rearrange("p g r -> p (g r)"),
-                scl[:].rearrange("p g r -> p (g r)"),
+                act_grouped[j][:].rearrange("p i g r j -> p (i g r j)"),
+                codes[:].rearrange("p i g r -> p (i g r)"),
+                scl[:].rearrange("p i g r -> p (i g r)"),
             )
-            act_codes[t] = codes
-            act_scales[t] = scl
+            act_codes[j] = codes
+            act_scales[j] = scl
 
         def mx(t):
             products[t] = []
@@ -403,8 +406,8 @@ def tile_temporalcrossattention_pa_kernel(tc, x, y, emb0, We, be, ln2_g, ln2_b, 
                 for g in range(PASSES):
                     nc.tensor.matmul_mx(
                         out=acc[:],
-                        lhsT=act_codes[t][:, g, :].bitcast(FP8X4),
-                        lhsT_scale=act_scales[t][:, g, :],
+                        lhsT=act_codes[t // 2][:, t % 2, g, :].bitcast(FP8X4),
+                        lhsT_scale=act_scales[t // 2][:, t % 2, g, :],
                         rhs=wo_codes[:, g, cols].bitcast(FP8X4),
                         rhs_scale=wo_scales[:, g, cols],
                         start=(g == 0),
@@ -419,7 +422,7 @@ def tile_temporalcrossattention_pa_kernel(tc, x, y, emb0, We, be, ln2_g, ln2_b, 
                 nc.vector.tensor_tensor(out=res[:, cols], in0=products[t][h][:], in1=residual[t][:, cols], op=ALU.add)
             nc.sync.dma_start(out=out[:, t, :], in_=res[:])
 
-        names = {"ld": ld, "pi": pi, "pe": pe, "sbn": sbn, "tr_e": tr_e, "silu_e": silu_e, "q_e": q_e, "vec": vec, "bn": bn, "agg": agg, "scales": scales, "rg": rg, "qw": qw,
+        names = {"sv": sv, "vec_t": vec_t, "vec_a": vec_a, "vec_b": vec_b, "ld": ld, "pi": pi, "pe": pe, "sbn": sbn, "tr_e": tr_e, "silu_e": silu_e, "q_e": q_e, "vec": vec, "bn": bn, "agg": agg, "scales": scales, "rg": rg, "qw": qw,
                  "product1": product1, "evac": evac, "tr_a": tr_a, "tr_c": tr_c, "copy_c": copy_c,
                  "xb": xb, "z": z, "mul": mul, "tr": tr, "silu": silu, "q": q, "mx": mx, "fin": fin}
         for op in CFG["ops"]:

@@ -87,7 +87,7 @@ def silu_out_of_psum(nc, pool, banks, tag="act_grouped"):
     return grouped
 
 
-CFG = {"dma":["y0-1","emb","y1-2","vec","y2-4","e0","y4-6","e1","e2","y6-8","e3","w0","y8-12","w1","bo","x0-4","y12-16","x4-8","x8-12","x12-16"],"ops":[["ld","y0-1"],["bn",0],["ld","emb"],["tr_e"],["silu_e"],["ld","y1-2"],["q_e"],["ld","vec"],["vec_t"],["vec_a"],["ld","y2-4"],["bn",1],["ld","e0"],["vec_b"],["rg","e0","S",0,640],["rg","e0","G",640,768],["ld","y4-6"],["agg",0],["rg","e0","G",768,896],["ld","e1"],["bn",2],["rg","e1","S",0,640],["rg","e0","G",896,1024],["ld","e2"],["vec"],["rg","e2","S",0,640],["rg","e1","G",640,768],["ld","y6-8"],["agg",1],["rg","e1","G",768,896],["ld","e3"],["bn",3],["rg","e1","G",896,1024],["ld","w0"],["agg",2],["rg","e2","G",640,768],["ld","y8-12"],["bn",4],["rg","e2","G",768,896],["ld","w1"],["agg",3],["sv",0,4],["rg","e2","G",896,1024],["ld","bo"],["qw","e0"],["scales",0,4],["ld","x0-4"],["agg",4],["rg","e3","G",640,768],["ld","y12-16"],["bn",5],["rg","e3","G",768,896],["ld","x4-8"],["bn",6],["rg","e3","G",896,1024],["ld","x8-12"],["agg",5],["qw","e1"],["product1",0],["agg",6],["evac",0,0,"a"],["bn",7],["evac",0,1,"a"],["tr_a"],["bn",8],["rg","e3","S",0,640],["ld","x12-16"],["agg",7],["sv",4,8],["scales",4,8],["qw","e2"],["z",0],["rg","w0","G",512,640],["agg",8],["evac",0,0,"l"],["rg","w0","G",640,768],["bn",9],["evac",0,1,"l"],["rg","w0","G",768,896],["bn",10],["rg","w0","S",0,512],["rg","w0","G",896,1024],["agg",9],["z",1],["rg","w1","G",512,640],["mul",0],["rg","w1","G",640,768],["agg",10],["rg","w1","G",768,896],["qw","e3"],["rg","w1","G",896,1024],["product1",1],["bn",11],["evac",1,0,"s"],["xb",0],["mul",1],["evac",1,1,"s"],["tr_c"],["agg",11],["copy_c"],["tr",0],["qw","w0"],["rg","w1","S",0,512],["bn",12],["sv",8,12],["scales",8,12],["agg",12],["silu",0],["xb",1],["tr",1],["qw","w1"],["silu",1],["xb",2],["q",0],["z",2],["xb",3],["mx",0],["mul",2],["z",3],["xb",4],["tr",2],["mul",3],["z",4],["xb",5],["fin",0],["z",5],["xb",6],["mul",4],["silu",2],["tr",3],["sbn",13],["mx",1],["fin",1],["silu",3],["xb",7],["tr",4],["bn",14],["z",6],["agg",14],["z",7],["mul",5],["silu",4],["tr",5],["q",1],["sbn",15],["mx",2],["mul",6],["sv",12,16],["scales",12,16],["mul",7],["silu",5],["fin",2],["z",8],["xb",8],["mx",3],["q",2],["z",9],["tr",6],["fin",3],["silu",6],["xb",9],["tr",7],["mul",8],["silu",7],["mx",4],["mul",9],["z",10],["fin",4],["z",11],["xb",10],["mx",5],["q",3],["tr",8],["fin",5],["silu",8],["xb",11],["tr",9],["mul",10],["silu",9],["mx",6],["mul",11],["z",12],["fin",6],["z",13],["xb",12],["mx",7],["q",4],["tr",10],["fin",7],["silu",10],["xb",13],["tr",11],["mul",12],["silu",11],["mx",8],["mul",13],["z",14],["fin",8],["z",15],["xb",14],["mx",9],["q",5],["tr",12],["fin",9],["silu",12],["xb",15],["tr",13],["mul",14],["silu",13],["mx",10],["mul",15],["fin",10],["mx",11],["q",6],["tr",14],["fin",11],["silu",14],["tr",15],["silu",15],["mx",12],["fin",12],["mx",13],["q",7],["fin",13],["mx",14],["fin",14],["mx",15],["fin",15]],"zb":6,"rb":4,"wg":3,"gg":1,"pre":[0,1,2,3,4,5,6,7,8,9,10,11,12,13,14,15],"pb":6,"mb":3,"xp":1,"vx":[],"whole":True,"pair":True}
+CFG = {"dma":["y0-1","emb","y1-2","vec","y2-4","e0","y4-6","e1","e2","y6-8","e3","y8-12","w0","y12-14","w1","y14-16","bo","x0-4","x4-8","x8-12","x12-16"],"ops":[["ld","y0-1"],["bn",0],["ld","emb"],["tr_e"],["silu_e"],["ld","y1-2"],["q_e"],["ld","vec"],["vec_t"],["vec_a"],["ld","y2-4"],["bn",1],["ld","e0"],["vec_b"],["rg","e0","S",0,640],["rg","e0","G",640,768],["ld","y4-6"],["agg",0],["rg","e0","G",768,896],["ld","e1"],["bn",2],["rg","e1","S",0,640],["rg","e0","G",896,1024],["ld","e2"],["vec"],["rg","e1","G",640,768],["ld","y6-8"],["agg",1],["rg","e1","G",768,896],["ld","e3"],["bn",3],["rg","e1","G",896,1024],["ld","y8-12"],["agg",2],["ld","w0"],["bn",4],["ld","y12-14"],["agg",3],["ld","w1"],["qw","e0"],["rg","e2","S",0,640],["rg","e2","G",640,768],["ld","y14-16"],["agg",4],["sv",0,4],["rg","e2","G",768,896],["ld","bo"],["bn",5],["rg","e2","G",896,1024],["ld","x0-4"],["bn",6],["scales",0,4],["ld","x4-8"],["agg",5],["ld","x8-12"],["qw","e1"],["rg","e3","G",640,768],["product1",0],["agg",6],["evac",0,0,"a"],["rg","e3","G",768,896],["bn",7],["evac",0,1,"a"],["rg","e3","G",896,1024],["tr_a"],["bn",8],["rg","e3","S",0,640],["ld","x12-16"],["agg",7],["sv",4,8],["scales",4,8],["bn",9],["z",0],["agg",8],["evac",0,0,"l"],["qw","e2"],["evac",0,1,"l"],["rg","w0","G",512,640],["agg",9],["rg","w0","S",0,512],["rg","w0","G",640,768],["bn",10],["z",1],["rg","w0","G",768,896],["bn",11],["rg","w0","G",896,1024],["agg",10],["mul",0],["agg",11],["qw","e3"],["rg","w1","G",512,640],["product1",1],["bn",12],["evac",1,0,"s"],["rg","w1","G",640,768],["mul",1],["evac",1,1,"s"],["rg","w1","G",768,896],["tr_c"],["agg",12],["copy_c"],["rg","w1","G",896,1024],["tr",0],["qw","w0"],["rg","w1","S",0,512],["xb",0],["bn",13],["sv",8,12],["scales",8,12],["bn",14],["silu",0],["xb",1],["tr",1],["agg",13],["z",2],["xb",2],["agg",14],["z",3],["xb",3],["bn",15],["silu",1],["agg",15],["z",4],["qw","w1"],["sv",12,16],["scales",12,16],["mul",2],["xb",4],["tr",2],["mul",3],["silu",2],["xb",5],["tr",3],["q",0],["z",5],["mx",0],["mul",4],["silu",3],["tr",4],["mul",5],["z",6],["fin",0],["silu",4],["xb",6],["mx",1],["q",1],["z",7],["tr",5],["mul",6],["silu",5],["fin",1],["z",8],["xb",7],["mx",2],["mul",7],["tr",6],["fin",2],["silu",6],["xb",8],["mx",3],["q",2],["z",9],["tr",7],["mul",8],["silu",7],["fin",3],["z",10],["xb",9],["mx",4],["mul",9],["tr",8],["fin",4],["silu",8],["xb",10],["mx",5],["q",3],["z",11],["tr",9],["mul",10],["silu",9],["fin",5],["z",12],["xb",11],["mx",6],["mul",11],["tr",10],["fin",6],["silu",10],["xb",12],["mx",7],["q",4],["z",13],["tr",11],["mul",12],["silu",11],["fin",7],["z",14],["xb",13],["mx",8],["mul",13],["tr",12],["fin",8],["silu",12],["xb",14],["mx",9],["q",5],["z",15],["tr",13],["mul",14],["silu",13],["fin",9],["xb",15],["mx",10],["mul",15],["tr",14],["fin",10],["silu",14],["mx",11],["q",6],["tr",15],["fin",11],["silu",15],["mx",12],["fin",12],["mx",13],["q",7],["fin",13],["mx",14],["fin",14],["mx",15],["fin",15]],"zb":7,"rb":4,"wg":2,"gg":1,"pre":[0,1,2,3,4,5,6,7,8,9,10,11,12,13,14,15],"pb":6,"mb":3,"xp":2,"vx":[],"whole":True,"pair":True}
 def tile_temporalcrossattention_pa_kernel(tc, x, y, emb0, We, be, ln2_g, ln2_b, Wo, bo, out):
     nc = tc.nc
     with ExitStack() as ctx:
@@ -113,6 +113,9 @@ def tile_temporalcrossattention_pa_kernel(tc, x, y, emb0, We, be, ln2_g, ln2_b, 
         make_identity(nc, ident[:])
         ident_bf = keep.tile([P, P], BF16)
         nc.vector.tensor_copy(out=ident_bf[:], in_=ident[:])
+        first_row = keep.tile([P, P], BF16)
+        nc.gpsimd.memset(first_row[:], 0.0)
+        nc.gpsimd.memset(first_row[0:1, :], 1.0)
         minus_half = keep.tile([P, LOAD_TILES], F32)
         nc.gpsimd.memset(minus_half[:], -0.5)
 
@@ -354,6 +357,25 @@ def tile_temporalcrossattention_pa_kernel(tc, x, y, emb0, We, be, ln2_g, ln2_b, 
                     out=residual[t][:, cols], in0=x_sb[t][:, cols], in1=bo_rows[:, cols], op=ALU.add,
                 )
 
+        def xt(t):
+            banks = []
+            for h in range(HALVES):
+                cols = slice(h * BANK, (h + 1) * BANK)
+                bank = psum_mm.tile([P, BANK], F32, tag="mm", name="x_bo")
+                nc.tensor.matmul(out=bank[:], lhsT=ident_bf[:], rhs=x_sb[t][:, cols], start=True, stop=False)
+                nc.tensor.matmul(out=bank[:], lhsT=first_row[:], rhs=bo_rows[:, cols], start=False, stop=True)
+                banks.append(bank)
+            st["xt", t] = banks
+
+        def xe(t, eng):
+            residual[t] = pre_pool.tile([P, D], F32, tag="pre", name="pre")
+            for h in range(HALVES):
+                cols = slice(h * BANK, (h + 1) * BANK)
+                if eng == "V":
+                    nc.vector.tensor_copy(out=residual[t][:, cols], in_=st["xt", t][h][:])
+                else:
+                    nc.scalar.copy(out=residual[t][:, cols], in_=st["xt", t][h][:])
+
         def z(t):
             nc.scalar.activation(
                 out=z_bias[:, t : t + 1], in_=neg_mean[:, t : t + 1], func=ACT.Identity, scale=rstd[:, t : t + 1]
@@ -422,7 +444,7 @@ def tile_temporalcrossattention_pa_kernel(tc, x, y, emb0, We, be, ln2_g, ln2_b, 
                 nc.vector.tensor_tensor(out=res[:, cols], in0=products[t][h][:], in1=residual[t][:, cols], op=ALU.add)
             nc.sync.dma_start(out=out[:, t, :], in_=res[:])
 
-        names = {"sv": sv, "vec_t": vec_t, "vec_a": vec_a, "vec_b": vec_b, "ld": ld, "pi": pi, "pe": pe, "sbn": sbn, "tr_e": tr_e, "silu_e": silu_e, "q_e": q_e, "vec": vec, "bn": bn, "agg": agg, "scales": scales, "rg": rg, "qw": qw,
+        names = {"xt": xt, "xe": xe, "sv": sv, "vec_t": vec_t, "vec_a": vec_a, "vec_b": vec_b, "ld": ld, "pi": pi, "pe": pe, "sbn": sbn, "tr_e": tr_e, "silu_e": silu_e, "q_e": q_e, "vec": vec, "bn": bn, "agg": agg, "scales": scales, "rg": rg, "qw": qw,
                  "product1": product1, "evac": evac, "tr_a": tr_a, "tr_c": tr_c, "copy_c": copy_c,
                  "xb": xb, "z": z, "mul": mul, "tr": tr, "silu": silu, "q": q, "mx": mx, "fin": fin}
         for op in CFG["ops"]:

@@ -23,9 +23,14 @@ CHUNKS = D // P
 BANK = 512
 HALVES = D // BANK
 W_COLS = 1024
-LOAD_TILES = 4
+GROUP = 2
+SCALES_TILES = 4
+WE_SCALAR_COLS = 640
+WO_SCALAR_COLS = 512
+X_TILES = 4
 BN_MAX = 512
 BN_DIM = 6
+MX_LAG = 3
 
 FLOPS = 2 * P * D * (2 * D) + 2 * (P * T) * D * D
 
@@ -36,22 +41,24 @@ def load_weight_piece(nc, pool, rows):
     return raw
 
 
-def regroup(nc, grouped, raw, engine, lo, hi):
-    if engine == "G":
+def regroup_weight_piece(nc, pool, raw, scalar_cols):
+    grouped = pool.tile([P, W_COLS, PACK], BF16, align_bytes=64, name="grouped")
+    nc.scalar.copy(
+        out=grouped[:, 0:scalar_cols, :].rearrange("p (c i) j -> p c j i", i=4),
+        in_=raw[:, :, 0:scalar_cols].rearrange("p j (c i) -> p c j i", i=4),
+    )
+    for first in range(scalar_cols, W_COLS, P):
+        cols = slice(first, first + P)
         nc.gpsimd.tensor_scalar(
-            out=grouped,
-            in0=raw[:, :, lo:hi].rearrange("p j n -> p n j"),
+            out=grouped[:, cols, :],
+            in0=raw[:, :, cols].rearrange("p j n -> p n j"),
             scalar1=1.0,
             scalar2=0.0,
             op0=ALU.mult,
             op1=ALU.add,
         )
-    else:
-        copy = nc.scalar.copy if engine == "S" else nc.vector.tensor_copy
-        copy(
-            out=grouped.rearrange("p (c i) j -> p c j i", i=4),
-            in_=raw[:, :, lo:hi].rearrange("p j (c i) -> p c j i", i=4),
-        )
+    return grouped
+
 
 def quantise(nc, grouped_flat, codes, scales):
     nc.vector.quantize_mx(out=codes.bitcast(FP8X4), scales=scales, in_=grouped_flat)
@@ -78,29 +85,24 @@ def transpose_rows(nc, psum, rows, addend, ident):
     return banks
 
 
-def silu_out_of_psum(nc, pool, banks, tag="act_grouped"):
-    grouped = pool.tile([P, PASSES, P, PACK], BF16, align_bytes=64, tag=tag, name="act_grouped")
+def silu_out_of_psum(nc, banks, grouped):
     for g in range(PASSES):
         nc.scalar.activation(
             out=grouped[:, g, :, :], in_=banks[g][:].rearrange("p j r -> p r j"), func=ACT.Silu
         )
-    return grouped
 
 
-CFG = {"dma":["y0-1","emb","y1-2","vec","y2-4","e0","y4-6","e1","e2","y6-8","e3","y8-12","w0","y12-14","w1","y14-16","bo","x0-4","x4-8","x8-12","x12-16"],"ops":[["ld","y0-1"],["bn",0],["ld","emb"],["tr_e"],["silu_e"],["ld","y1-2"],["q_e"],["ld","vec"],["vec_t"],["vec_a"],["ld","y2-4"],["bn",1],["ld","e0"],["vec_b"],["rg","e0","S",0,640],["rg","e0","G",640,768],["ld","y4-6"],["agg",0],["rg","e0","G",768,896],["ld","e1"],["bn",2],["rg","e1","S",0,640],["rg","e0","G",896,1024],["ld","e2"],["vec"],["rg","e1","G",640,768],["ld","y6-8"],["agg",1],["rg","e1","G",768,896],["ld","e3"],["bn",3],["rg","e1","G",896,1024],["ld","y8-12"],["agg",2],["ld","w0"],["bn",4],["ld","y12-14"],["agg",3],["ld","w1"],["qw","e0"],["rg","e2","S",0,640],["rg","e2","G",640,768],["ld","y14-16"],["agg",4],["sv",0,4],["rg","e2","G",768,896],["ld","bo"],["bn",5],["rg","e2","G",896,1024],["ld","x0-4"],["bn",6],["scales",0,4],["ld","x4-8"],["agg",5],["ld","x8-12"],["qw","e1"],["rg","e3","G",640,768],["product1",0],["agg",6],["evac",0,0,"a"],["rg","e3","G",768,896],["bn",7],["evac",0,1,"a"],["rg","e3","G",896,1024],["tr_a"],["bn",8],["rg","e3","S",0,640],["ld","x12-16"],["agg",7],["sv",4,8],["scales",4,8],["bn",9],["z",0],["agg",8],["evac",0,0,"l"],["qw","e2"],["evac",0,1,"l"],["rg","w0","G",512,640],["agg",9],["rg","w0","S",0,512],["rg","w0","G",640,768],["bn",10],["z",1],["rg","w0","G",768,896],["bn",11],["rg","w0","G",896,1024],["agg",10],["mul",0],["agg",11],["qw","e3"],["rg","w1","G",512,640],["product1",1],["bn",12],["evac",1,0,"s"],["rg","w1","G",640,768],["mul",1],["evac",1,1,"s"],["rg","w1","G",768,896],["tr_c"],["agg",12],["copy_c"],["rg","w1","G",896,1024],["tr",0],["qw","w0"],["rg","w1","S",0,512],["xb",0],["bn",13],["sv",8,12],["scales",8,12],["bn",14],["silu",0],["xb",1],["tr",1],["agg",13],["z",2],["xb",2],["agg",14],["z",3],["xb",3],["bn",15],["silu",1],["agg",15],["z",4],["qw","w1"],["sv",12,16],["scales",12,16],["mul",2],["xb",4],["tr",2],["mul",3],["silu",2],["xb",5],["tr",3],["q",0],["z",5],["mx",0],["mul",4],["silu",3],["tr",4],["mul",5],["z",6],["fin",0],["silu",4],["xb",6],["mx",1],["q",1],["z",7],["tr",5],["mul",6],["silu",5],["fin",1],["z",8],["xb",7],["mx",2],["mul",7],["tr",6],["fin",2],["silu",6],["xb",8],["mx",3],["q",2],["z",9],["tr",7],["mul",8],["silu",7],["fin",3],["z",10],["xb",9],["mx",4],["mul",9],["tr",8],["fin",4],["silu",8],["xb",10],["mx",5],["q",3],["z",11],["tr",9],["mul",10],["silu",9],["fin",5],["z",12],["xb",11],["mx",6],["mul",11],["tr",10],["fin",6],["silu",10],["xb",12],["mx",7],["q",4],["z",13],["tr",11],["mul",12],["silu",11],["fin",7],["z",14],["xb",13],["mx",8],["mul",13],["tr",12],["fin",8],["silu",12],["xb",14],["mx",9],["q",5],["z",15],["tr",13],["mul",14],["silu",13],["fin",9],["xb",15],["mx",10],["mul",15],["tr",14],["fin",10],["silu",14],["mx",11],["q",6],["tr",15],["fin",11],["silu",15],["mx",12],["fin",12],["mx",13],["q",7],["fin",13],["mx",14],["fin",14],["mx",15],["fin",15]],"zb":7,"rb":4,"wg":2,"gg":1,"pre":[0,1,2,3,4,5,6,7,8,9,10,11,12,13,14,15],"pb":6,"mb":3,"xp":2,"vx":[],"whole":True,"pair":True}
 def tile_temporalcrossattention_pa_kernel(tc, x, y, emb0, We, be, ln2_g, ln2_b, Wo, bo, out):
     nc = tc.nc
     with ExitStack() as ctx:
         keep = ctx.enter_context(tc.tile_pool(name="keep", bufs=1))
         we_raw_pool = ctx.enter_context(tc.tile_pool(name="we_raw", bufs=2 * PASSES))
         wo_raw_pool = ctx.enter_context(tc.tile_pool(name="wo_raw", bufs=PASSES))
-        w_grouped_pool = ctx.enter_context(tc.tile_pool(name="w_grouped", bufs=CFG["wg"]))
-        gp_grouped_pool = ctx.enter_context(tc.tile_pool(name="gp_grouped", bufs=CFG["gg"]))
-        z_pool = ctx.enter_context(tc.tile_pool(name="z", bufs=CFG["zb"]))
+        w_grouped_pool = ctx.enter_context(tc.tile_pool(name="w_grouped", bufs=2))
+        z_pool = ctx.enter_context(tc.tile_pool(name="z", bufs=7))
         act_pool = ctx.enter_context(tc.tile_pool(name="act", bufs=3))
-        res_pool = ctx.enter_context(tc.tile_pool(name="res", bufs=CFG["rb"]))
-        mix_pool = ctx.enter_context(tc.tile_pool(name="mix", bufs=CFG["mb"]))
-        pre_pool = ctx.enter_context(tc.tile_pool(name="pre", bufs=CFG["pb"]))
+        res_pool = ctx.enter_context(tc.tile_pool(name="res", bufs=4))
+        x_bo_pool = ctx.enter_context(tc.tile_pool(name="x_bo", bufs=6))
         small = ctx.enter_context(tc.tile_pool(name="small", bufs=4))
         psum_keep = ctx.enter_context(tc.psum_pool(name="psum_keep", bufs=HALVES))
         psum_t = ctx.enter_context(tc.psum_pool(name="psum_t", bufs=3))
@@ -113,54 +115,68 @@ def tile_temporalcrossattention_pa_kernel(tc, x, y, emb0, We, be, ln2_g, ln2_b, 
         make_identity(nc, ident[:])
         ident_bf = keep.tile([P, P], BF16)
         nc.vector.tensor_copy(out=ident_bf[:], in_=ident[:])
-        first_row = keep.tile([P, P], BF16)
-        nc.gpsimd.memset(first_row[:], 0.0)
-        nc.gpsimd.memset(first_row[0:1, :], 1.0)
-        minus_half = keep.tile([P, LOAD_TILES], F32)
+        minus_half = keep.tile([P, SCALES_TILES], F32)
         nc.gpsimd.memset(minus_half[:], -0.5)
+        eps = keep.tile([P, 1], F32)
+        nc.gpsimd.memset(eps[:], 0.0)
+        nc.gpsimd.tensor_scalar(out=eps[:], in0=eps[:], scalar1=1.0, scalar2=EPS, op0=ALU.mult, op1=ALU.add)
 
-        def load_tiles(src, c, name):
-            part = keep.tile([P, LOAD_TILES, D], BF16, name=name % c)
-            nc.sync.dma_start(out=part[:], in_=src[:, c * LOAD_TILES : (c + 1) * LOAD_TILES, :])
-            return part
-
+        y_tiles = {}
+        x_tiles = {}
         emb_raw = keep.tile([P, D], BF16)
-        y_sb = {}
-        x_sb = {}
-        we_raw = {}
-        wo_raw = {}
         bo_rows = keep.tile([P, D], BF16)
-        def ld(item):
-            if item == "emb":
-                nc.sync.dma_start(out=emb_raw[:], in_=emb0)
-            elif item == "vec":
-                nc.sync.dma_start(out=vec_rows[0:16, :], in_=be.rearrange("(r c) -> r c", c=P))
-                nc.sync.dma_start(out=vec_rows[16:24, :], in_=ln2_g.rearrange("(r c) -> r c", c=P))
-                nc.sync.dma_start(out=vec_rows[24:32, :], in_=ln2_b.rearrange("(r c) -> r c", c=P))
-            elif item == "bo":
-                nc.sync.dma_start(out=bo_rows[:], in_=bo.partition_broadcast(P))
-            elif item[0] in "xy":
-                lo, hi = [int(v) for v in item[1:].split("-")]
-                if item[0] == "x":
-                    part = we_raw_pool.tile([P, PACK, W_COLS], BF16, tag="raw", name="x_" + str(lo))
-                else:
-                    part = keep.tile([P, hi - lo, D], BF16, name=item[0] + "_" + str(lo))
-                nc.sync.dma_start(out=part[:], in_=(y if item[0] == "y" else x)[:, lo:hi, :])
-                for t in range(lo, hi):
-                    (y_sb if item[0] == "y" else x_sb)[t] = part[:, t - lo, :]
-            elif item[0] == "e":
-                c = int(item[1])
-                side, g = divmod(c, PASSES)
-                we_raw[c] = load_weight_piece(
-                    nc, we_raw_pool,
-                    We[g * K_PASS : (g + 1) * K_PASS, side * W_COLS : (side + 1) * W_COLS],
-                )
-            else:
-                g = int(item[1])
-                wo_raw[g] = load_weight_piece(nc, wo_raw_pool, Wo[g * K_PASS : (g + 1) * K_PASS, :])
+
+        def load_y(lo, hi):
+            part = keep.tile([P, hi - lo, D], BF16, name="y_%d" % lo)
+            nc.sync.dma_start(out=part[:], in_=y[:, lo:hi, :])
+            for t in range(lo, hi):
+                y_tiles[t] = part[:, t - lo, :]
+
+        def load_x(lo):
+            part = we_raw_pool.tile([P, X_TILES, D], BF16, tag="raw", name="x_part")
+            nc.sync.dma_start(out=part[:], in_=x[:, lo : lo + X_TILES, :])
+            for t in range(lo, lo + X_TILES):
+                x_tiles[t] = part[:, t - lo, :]
+
+        def load_we(side, g):
+            cols = slice(side * W_COLS, (side + 1) * W_COLS)
+            return load_weight_piece(nc, we_raw_pool, We[g * K_PASS : (g + 1) * K_PASS, cols])
+
+        def load_wo(g):
+            return load_weight_piece(nc, wo_raw_pool, Wo[g * K_PASS : (g + 1) * K_PASS, :])
+
+        load_y(0, 1)
+        nc.sync.dma_start(out=emb_raw[:], in_=emb0)
+        load_y(1, 2)
+        nc.sync.dma_start(out=vec_rows[0:16, :], in_=be.rearrange("(r c) -> r c", c=P))
+        nc.sync.dma_start(out=vec_rows[16:24, :], in_=ln2_g.rearrange("(r c) -> r c", c=P))
+        nc.sync.dma_start(out=vec_rows[24:32, :], in_=ln2_b.rearrange("(r c) -> r c", c=P))
+        load_y(2, 4)
+        we_raw = {}
+        we_raw[0, 0] = load_we(0, 0)
+        load_y(4, 6)
+        we_raw[0, 1] = load_we(0, 1)
+        we_raw[1, 0] = load_we(1, 0)
+        load_y(6, 8)
+        we_raw[1, 1] = load_we(1, 1)
+        load_y(8, 12)
+        wo_raw = [load_wo(0)]
+        load_y(12, 14)
+        wo_raw.append(load_wo(1))
+        load_y(14, 16)
+        nc.sync.dma_start(out=bo_rows[:], in_=bo.partition_broadcast(P))
 
         emb_codes = keep.tile([P, PASSES, P], U32, align_bytes=64)
         emb_scales = keep.tile([P, PASSES, P], U8, align_bytes=64)
+        we_codes = keep.tile([P, 2, PASSES, W_COLS], U32, align_bytes=64)
+        we_scales = keep.tile([P, 2, PASSES, W_COLS], U8, align_bytes=64)
+        wo_codes = keep.tile([P, PASSES, W_COLS], U32, align_bytes=64)
+        wo_scales = keep.tile([P, PASSES, W_COLS], U8, align_bytes=64)
+        mean_var = keep.tile([P, T, 2], F32)
+        var_eps = keep.tile([P, T], F32)
+        neg_mean = keep.tile([P, T], F32)
+        rstd = keep.tile([P, T], F32)
+        z_bias = keep.tile([P, T], F32)
         vec_cols = keep.tile([P, 4 * CHUNKS], F32)
         be_scale = vec_cols[:, 0:CHUNKS]
         be_shift = vec_cols[:, CHUNKS : 2 * CHUNKS]
@@ -168,169 +184,65 @@ def tile_temporalcrossattention_pa_kernel(tc, x, y, emb0, We, be, ln2_g, ln2_b, 
         beta = vec_cols[:, 3 * CHUNKS : 4 * CHUNKS]
         a_bias = keep.tile([P, CHUNKS], F32)
         c_bias = keep.tile([P, CHUNKS], F32)
-        mean_var = keep.tile([P, T, 2], F32)
-        rstd = keep.tile([P, T], F32)
-        z_bias = keep.tile([P, T], F32)
-        var_eps = keep.tile([P, T], F32)
-        neg_mean = keep.tile([P, T], F32)
-        eps_col = keep.tile([P, 1], F32)
-        nc.gpsimd.memset(eps_col[:], 0.0)
-        nc.gpsimd.tensor_scalar(out=eps_col[:], in0=eps_col[:], scalar1=1.0, scalar2=EPS, op0=ALU.mult, op1=ALU.add)
-        we_codes = keep.tile([P, 2 * PASSES, W_COLS], U32, align_bytes=64)
-        we_scales = keep.tile([P, 2 * PASSES, W_COLS], U8, align_bytes=64)
-        wo_codes = keep.tile([P, PASSES, W_COLS], U32, align_bytes=64)
-        wo_scales = keep.tile([P, PASSES, W_COLS], U8, align_bytes=64)
         a_t = res_pool.tile([P, D], F32, tag="res", name="a_t")
         l_t = res_pool.tile([P, D], F32, tag="res", name="l_t")
         s_t = res_pool.tile([P, D], F32, tag="res", name="s_t")
         c_rows = keep.tile([P, D], F32)
-        st = {"stats": {}}
-        grouped = {}
-        e_banks = {}
 
-        def tr_e():
-            st["e"] = transpose_rows(nc, psum_t, emb_raw, None, ident_bf)
+        stats = {}
 
-        def silu_e():
-            st["eg"] = silu_out_of_psum(nc, act_pool, st["e"])
+        def moments(*tiles):
+            for t in tiles:
+                stats[t] = small.tile([P, D // BN_MAX, BN_DIM], F32, name="stats")
+                for s in range(D // BN_MAX):
+                    nc.vector.bn_stats(out=stats[t][:, s, :], in_=y_tiles[t][:, s * BN_MAX : (s + 1) * BN_MAX])
+                if t > 0:
+                    aggregate(t - 1)
 
-        def q_e():
-            quantise(
-                nc,
-                st["eg"][:].rearrange("p g r j -> p (g r j)"),
-                emb_codes[:].rearrange("p g r -> p (g r)"),
-                emb_scales[:].rearrange("p g r -> p (g r)"),
-            )
+        def aggregate(t):
+            nc.vector.bn_aggr(out=mean_var[:, t, :], in_=stats[t][:].rearrange("p s k -> p (s k)"))
 
-        def vec_t():
-            bank = psum_mm.tile([P, PACK, P], BF16, tag="mm", name="vec_bank")
-            nc.tensor.transpose(out=bank[:, 0, :], in_=vec_rows[:], identity=ident_bf[:])
-            st["vec"] = bank
+        def prepare_scales(first):
+            tiles = slice(first, first + SCALES_TILES)
+            nc.scalar.activation(out=var_eps[:, tiles], in_=mean_var[:, tiles, 1], func=ACT.Identity, bias=eps[:])
+            nc.scalar.mul(neg_mean[:, tiles], mean_var[:, tiles, 0], -1.0)
 
-        def vec_a():
-            nc.vector.tensor_copy(out=vec_cols[:], in_=st["vec"][:, 0, 0 : 4 * CHUNKS])
+        def make_scales(first):
+            tiles = slice(first, first + SCALES_TILES)
+            nc.gpsimd.tensor_tensor(out=rstd[:, tiles], in0=var_eps[:, tiles], in1=minus_half[:], op=ALU.pow)
 
-        def vec_b():
-            nc.vector.scalar_tensor_tensor(
-                out=a_bias[:], in0=be_scale, scalar=1.0, in1=gain, op0=ALU.add, op1=ALU.mult
-            )
-            nc.vector.scalar_tensor_tensor(
-                out=c_bias[:], in0=be_scale, scalar=1.0, in1=beta, op0=ALU.add, op1=ALU.mult
-            )
+        def quantise_weight_piece(grouped, codes, scales):
+            quantise(nc, grouped[:].rearrange("p n j -> p (n j)"), codes, scales)
 
-        def vec():
-            nc.vector.tensor_tensor(out=c_bias[:], in0=c_bias[:], in1=be_shift, op=ALU.add)
-
-        def sbn(t):
-            src = y_sb[t]
-            total = small.tile([P, 1], F32, name="total")
-            junk = keep.tile([P, D], BF16, name="junk") if "junk" not in st else st["junk"]
-            st["junk"] = junk
-            nc.scalar.activation(out=junk[:], in_=src, func=ACT.Identity, accum_out=total[:])
-            shift = small.tile([P, 1], F32, name="shift")
-            nc.scalar.mul(shift[:], total[:], 1.0 / (32.0 * D))
-            nc.scalar.mul(mean_var[:, t, 0:1], total[:], 1.0 / D)
-            nc.scalar.activation(
-                out=junk[:], in_=src, func=ACT.Square, scale=-1.0 / 32.0, bias=shift[:],
-                accum_out=mean_var[:, t, 1:2],
-            )
-
-        def bn(t):
-            stats = small.tile([P, D // BN_MAX, BN_DIM], F32, name="stats")
-            for s in range(D // BN_MAX):
-                nc.vector.bn_stats(
-                    out=stats[:, s, :], in_=y_sb[t][:, s * BN_MAX : (s + 1) * BN_MAX]
-                )
-            st["stats"][t] = stats
-
-        def agg(t):
-            nc.vector.bn_aggr(
-                out=mean_var[:, t, :], in_=st["stats"][t][:].rearrange("p s k -> p (s k)")
-            )
-
-        def sv(lo, hi):
-            nc.scalar.activation(out=var_eps[:, lo:hi], in_=mean_var[:, lo:hi, 1], func=ACT.Identity, bias=eps_col[:])
-            nc.scalar.mul(neg_mean[:, lo:hi], mean_var[:, lo:hi, 0], -1.0)
-
-        def scales(lo, hi):
-            nc.gpsimd.tensor_tensor(out=rstd[:, lo:hi], in0=var_eps[:, lo:hi], in1=minus_half[:, 0 : hi - lo], op=ALU.pow)
-
-        def rg(name, eng, lo, hi):
-            if name not in grouped:
-                grouped[name] = w_grouped_pool.tile([P, W_COLS, PACK], BF16, align_bytes=64, name="grouped")
-            raw = we_raw[int(name[1])] if name[0] == "e" else wo_raw[int(name[1])]
-            regroup(nc, grouped[name][:, lo:hi, :], raw, eng, lo, hi)
-
-        def pi(name, lo, hi):
-            raw = we_raw[int(name[1])] if name[0] == "e" else wo_raw[int(name[1])]
-            bank = psum_t.tile([P, hi - lo, PACK], BF16, tag="kT", name="il")
-            for a in range(0, hi - lo, P):
-                nc.tensor.matmul(
-                    out=bank[:, a : a + P, :], lhsT=ident_bf[:],
-                    rhs=raw[:, :, lo + a : lo + a + P].rearrange("p j n -> p n j"), start=True, stop=True,
-                )
-            st["il", name, lo] = bank
-
-        def pe(name, eng, lo, hi, base, top):
-            if (name, base) not in grouped:
-                grouped[name, base] = w_grouped_pool.tile([P, top - base, PACK], BF16, align_bytes=64, name="wp_" + str(top - base))
-            dst = grouped[name, base][:, lo - base : hi - base, :]
-            if eng == "S":
-                nc.scalar.copy(out=dst, in_=st["il", name, lo][:])
-            else:
-                nc.vector.tensor_copy(out=dst, in_=st["il", name, lo][:])
-
-        def qw(name):
-            c = int(name[1])
-            codes, scl = (we_codes, we_scales) if name[0] == "e" else (wo_codes, wo_scales)
-            quantise(nc, grouped[name][:].rearrange("p n j -> p (n j)"), codes[:, c, :], scl[:, c, :])
-
-        def product1(side):
+        def first_product(side):
+            banks = []
             for h in range(HALVES):
-                e_bank = psum_mm.tile([P, PACK, P], F32, tag="mm", name="e_bank")
+                bank = psum_mm.tile([P, PACK, P], F32, tag="mm", name="e_bank")
                 for i in range(PACK):
                     cols = slice(h * BANK + i * P, h * BANK + (i + 1) * P)
                     for g in range(PASSES):
                         nc.tensor.matmul_mx(
-                            out=e_bank[:, i, :],
-                            lhsT=we_codes[:, side * PASSES + g, cols].bitcast(FP8X4),
-                            lhsT_scale=we_scales[:, side * PASSES + g, cols],
+                            out=bank[:, i, :],
+                            lhsT=we_codes[:, side, g, cols].bitcast(FP8X4),
+                            lhsT_scale=we_scales[:, side, g, cols],
                             rhs=emb_codes[:, g, :].bitcast(FP8X4),
                             rhs_scale=emb_scales[:, g, :],
                             start=(g == 0),
                             stop=(g == PASSES - 1),
                         )
-                e_banks[side, h] = e_bank
+                banks.append(bank)
+            return banks
 
-        def evac(side, h, what):
-            for i in range(PACK):
-                k = h * PACK + i
-                cols = slice(k * P, (k + 1) * P)
-                src = e_banks[side, h][:, i, :]
-                if what == "a":
-                    nc.scalar.activation(
-                        out=a_t[:, cols], in_=src, func=ACT.Identity,
-                        scale=gain[:, k : k + 1], bias=a_bias[:, k : k + 1],
-                    )
-                elif what == "l":
-                    nc.scalar.activation(
-                        out=l_t[:, cols], in_=src, func=ACT.Identity, scale=beta[:, k : k + 1]
-                    )
-                else:
-                    nc.scalar.activation(
-                        out=s_t[:, cols], in_=src, func=ACT.Identity, bias=c_bias[:, k : k + 1]
-                    )
-
-        def tr_a():
-            st["a"] = transpose_rows(nc, psum_keep, a_t, None, ident)
-
-        def tr_c():
-            st["c"] = transpose_rows(nc, psum_t, s_t, l_t, ident)
-
-        def copy_c():
-            for h in range(HALVES):
-                nc.scalar.copy(
-                    out=c_rows[:, h * BANK : (h + 1) * BANK], in_=st["c"][h][:].rearrange("p i d -> p (i d)")
+        def out_of_banks(table, banks, scale, bias):
+            for k in range(CHUNKS):
+                factors = {}
+                if scale is not None:
+                    factors["scale"] = scale[:, k : k + 1]
+                if bias is not None:
+                    factors["bias"] = bias[:, k : k + 1]
+                nc.scalar.activation(
+                    out=table[:, k * P : (k + 1) * P], in_=banks[k // PACK][:, k % PACK, :],
+                    func=ACT.Identity, **factors,
                 )
 
         z_tiles = {}
@@ -339,88 +251,51 @@ def tile_temporalcrossattention_pa_kernel(tc, x, y, emb0, We, be, ln2_g, ln2_b, 
         act_codes = {}
         act_scales = {}
         products = {}
-        residual = {}
+        x_bo = {}
 
-        def xb(t):
-            if t in CFG["pre"]:
-                residual[t] = pre_pool.tile([P, D], F32, tag="pre", name="pre")
-            else:
-                residual[t] = mix_pool.tile([P, D], F32, align_bytes=64, tag="mix", name="xbo")
-            w = D // CFG["xp"]
-            if t in CFG["vx"]:
-                for i in range(1):
-                    nc.vector.tensor_tensor(out=residual[t][:], in0=x_sb[t], in1=bo_rows[:], op=ALU.add)
-                return
-            for i in range(CFG["xp"]):
-                cols = slice(i * w, (i + 1) * w)
-                nc.gpsimd.tensor_tensor(
-                    out=residual[t][:, cols], in0=x_sb[t][:, cols], in1=bo_rows[:, cols], op=ALU.add,
-                )
-
-        def xt(t):
-            banks = []
-            for h in range(HALVES):
-                cols = slice(h * BANK, (h + 1) * BANK)
-                bank = psum_mm.tile([P, BANK], F32, tag="mm", name="x_bo")
-                nc.tensor.matmul(out=bank[:], lhsT=ident_bf[:], rhs=x_sb[t][:, cols], start=True, stop=False)
-                nc.tensor.matmul(out=bank[:], lhsT=first_row[:], rhs=bo_rows[:, cols], start=False, stop=True)
-                banks.append(bank)
-            st["xt", t] = banks
-
-        def xe(t, eng):
-            residual[t] = pre_pool.tile([P, D], F32, tag="pre", name="pre")
-            for h in range(HALVES):
-                cols = slice(h * BANK, (h + 1) * BANK)
-                if eng == "V":
-                    nc.vector.tensor_copy(out=residual[t][:, cols], in_=st["xt", t][h][:])
-                else:
-                    nc.scalar.copy(out=residual[t][:, cols], in_=st["xt", t][h][:])
-
-        def z(t):
+        def normalise(t):
             nc.scalar.activation(
                 out=z_bias[:, t : t + 1], in_=neg_mean[:, t : t + 1], func=ACT.Identity, scale=rstd[:, t : t + 1]
             )
-            zt = z_pool.tile([P, D], F32, tag="z", name="z")
+            z = z_pool.tile([P, D], F32, tag="z", name="z")
             nc.scalar.activation(
-                out=zt[:], in_=y_sb[t], func=ACT.Identity,
-                scale=rstd[:, t : t + 1], bias=z_bias[:, t : t + 1],
+                out=z[:], in_=y_tiles[t], func=ACT.Identity, scale=rstd[:, t : t + 1], bias=z_bias[:, t : t + 1]
             )
-            z_tiles[t] = zt
+            z_tiles[t] = z
 
-        def mul(t):
-            zt = z_tiles[t]
+        def modulate(t):
+            z = z_tiles[t]
             for h in range(HALVES):
                 cols = slice(h * BANK, (h + 1) * BANK)
                 nc.vector.tensor_tensor(
-                    out=zt[:, cols], in0=zt[:, cols], in1=st["a"][h][:].rearrange("p i d -> p (i d)"),
-                    op=ALU.mult,
+                    out=z[:, cols], in0=z[:, cols], in1=a_banks[h][:].rearrange("p i d -> p (i d)"), op=ALU.mult
                 )
 
-        def tr(t):
+        def transpose(t):
             h_banks[t] = transpose_rows(nc, psum_t, z_tiles[t], c_rows, ident)
 
-        def silu(t):
-            j, i = divmod(t, 2)
+        def activate(t):
+            group, i = divmod(t, GROUP)
             if i == 0:
-                act_grouped[j] = act_pool.tile([P, 2, PASSES, P, PACK], BF16, align_bytes=64, tag="act_pair", name="act_pair")
-            for g in range(PASSES):
-                nc.scalar.activation(
-                    out=act_grouped[j][:, i, g, :, :], in_=h_banks[t][g][:].rearrange("p j r -> p r j"), func=ACT.Silu
+                act_grouped[group] = act_pool.tile(
+                    [P, GROUP, PASSES, P, PACK], BF16, align_bytes=64, tag="act_grouped", name="act_grouped"
                 )
+            silu_out_of_psum(nc, h_banks[t], act_grouped[group][:, i, :, :, :])
 
-        def q(j):
-            codes = act_pool.tile([P, 2, PASSES, P], U32, align_bytes=64, tag="act_codes", name="act_codes")
-            scl = act_pool.tile([P, 2, PASSES, P], U8, align_bytes=64, tag="act_scales", name="act_scales")
+        def quantise_group(group):
+            codes = act_pool.tile([P, GROUP, PASSES, P], U32, align_bytes=64, tag="act_codes", name="act_codes")
+            scales = act_pool.tile([P, GROUP, PASSES, P], U8, align_bytes=64, tag="act_scales", name="act_scales")
             quantise(
                 nc,
-                act_grouped[j][:].rearrange("p i g r j -> p (i g r j)"),
+                act_grouped[group][:].rearrange("p i g r j -> p (i g r j)"),
                 codes[:].rearrange("p i g r -> p (i g r)"),
-                scl[:].rearrange("p i g r -> p (i g r)"),
+                scales[:].rearrange("p i g r -> p (i g r)"),
             )
-            act_codes[j] = codes
-            act_scales[j] = scl
+            act_codes[group] = codes
+            act_scales[group] = scales
 
-        def mx(t):
+        def project(t):
+            group, i = divmod(t, GROUP)
             products[t] = []
             for h in range(HALVES):
                 cols = slice(h * BANK, (h + 1) * BANK)
@@ -428,8 +303,8 @@ def tile_temporalcrossattention_pa_kernel(tc, x, y, emb0, We, be, ln2_g, ln2_b, 
                 for g in range(PASSES):
                     nc.tensor.matmul_mx(
                         out=acc[:],
-                        lhsT=act_codes[t // 2][:, t % 2, g, :].bitcast(FP8X4),
-                        lhsT_scale=act_scales[t // 2][:, t % 2, g, :],
+                        lhsT=act_codes[group][:, i, g, :].bitcast(FP8X4),
+                        lhsT_scale=act_scales[group][:, i, g, :],
                         rhs=wo_codes[:, g, cols].bitcast(FP8X4),
                         rhs_scale=wo_scales[:, g, cols],
                         start=(g == 0),
@@ -437,15 +312,104 @@ def tile_temporalcrossattention_pa_kernel(tc, x, y, emb0, We, be, ln2_g, ln2_b, 
                     )
                 products[t].append(acc)
 
-        def fin(t):
+        def add_bias_to_residual(t):
+            x_bo[t] = x_bo_pool.tile([P, D], F32, tag="x_bo", name="x_bo")
+            for h in range(HALVES):
+                cols = slice(h * BANK, (h + 1) * BANK)
+                nc.gpsimd.tensor_tensor(
+                    out=x_bo[t][:, cols], in0=x_tiles[t][:, cols], in1=bo_rows[:, cols], op=ALU.add
+                )
+
+        def finish(t):
             res = res_pool.tile([P, D], F32, tag="res", name="res")
             for h in range(HALVES):
                 cols = slice(h * BANK, (h + 1) * BANK)
-                nc.vector.tensor_tensor(out=res[:, cols], in0=products[t][h][:], in1=residual[t][:, cols], op=ALU.add)
-            nc.sync.dma_start(out=out[:, t, :], in_=res[:])
+                nc.vector.tensor_tensor(out=res[:, cols], in0=products[t][h][:], in1=x_bo[t][:, cols], op=ALU.add)
+                if t == T - 1:
+                    nc.sync.dma_start(out=out[:, t, cols], in_=res[:, cols])
+            if t < T - 1:
+                nc.sync.dma_start(out=out[:, t, :], in_=res[:])
 
-        names = {"xt": xt, "xe": xe, "sv": sv, "vec_t": vec_t, "vec_a": vec_a, "vec_b": vec_b, "ld": ld, "pi": pi, "pe": pe, "sbn": sbn, "tr_e": tr_e, "silu_e": silu_e, "q_e": q_e, "vec": vec, "bn": bn, "agg": agg, "scales": scales, "rg": rg, "qw": qw,
-                 "product1": product1, "evac": evac, "tr_a": tr_a, "tr_c": tr_c, "copy_c": copy_c,
-                 "xb": xb, "z": z, "mul": mul, "tr": tr, "silu": silu, "q": q, "mx": mx, "fin": fin}
-        for op in CFG["ops"]:
-            names[op[0]](*op[1:])
+        moments(0)
+        emb_banks = transpose_rows(nc, psum_t, emb_raw, None, ident_bf)
+        emb_grouped = act_pool.tile([P, PASSES, P, PACK], BF16, align_bytes=64, tag="emb_grouped", name="emb_grouped")
+        silu_out_of_psum(nc, emb_banks, emb_grouped[:])
+        quantise(
+            nc,
+            emb_grouped[:].rearrange("p g r j -> p (g r j)"),
+            emb_codes[:].rearrange("p g r -> p (g r)"),
+            emb_scales[:].rearrange("p g r -> p (g r)"),
+        )
+        vec_bank = psum_mm.tile([P, PACK, P], BF16, tag="mm", name="vec_bank")
+        nc.tensor.transpose(out=vec_bank[:, 0, :], in_=vec_rows[:], identity=ident_bf[:])
+        nc.vector.tensor_copy(out=vec_cols[:], in_=vec_bank[:, 0, 0 : 4 * CHUNKS])
+        moments(1)
+        nc.vector.scalar_tensor_tensor(out=a_bias[:], in0=be_scale, scalar=1.0, in1=gain, op0=ALU.add, op1=ALU.mult)
+        nc.vector.scalar_tensor_tensor(out=c_bias[:], in0=be_scale, scalar=1.0, in1=beta, op0=ALU.add, op1=ALU.mult)
+        nc.vector.tensor_tensor(out=c_bias[:], in0=c_bias[:], in1=be_shift, op=ALU.add)
+        moments(2, 3, 4)
+
+        we_grouped = regroup_weight_piece(nc, w_grouped_pool, we_raw[0, 0], WE_SCALAR_COLS)
+        quantise_weight_piece(we_grouped, we_codes[:, 0, 0, :], we_scales[:, 0, 0, :])
+        we_grouped = regroup_weight_piece(nc, w_grouped_pool, we_raw[0, 1], WE_SCALAR_COLS)
+        moments(5, 6)
+        quantise_weight_piece(we_grouped, we_codes[:, 0, 1, :], we_scales[:, 0, 1, :])
+        e_banks = first_product(0)
+        we_grouped = regroup_weight_piece(nc, w_grouped_pool, we_raw[1, 0], WE_SCALAR_COLS)
+        prepare_scales(0)
+        make_scales(0)
+        moments(7, 8, 9)
+        out_of_banks(a_t, e_banks, gain, a_bias)
+        quantise_weight_piece(we_grouped, we_codes[:, 1, 0, :], we_scales[:, 1, 0, :])
+        a_banks = transpose_rows(nc, psum_keep, a_t, None, ident)
+        we_grouped = regroup_weight_piece(nc, w_grouped_pool, we_raw[1, 1], WE_SCALAR_COLS)
+        prepare_scales(4)
+        make_scales(4)
+        for first in range(0, T, X_TILES):
+            load_x(first)
+        normalise(0)
+        moments(10, 11)
+        modulate(0)
+        out_of_banks(l_t, e_banks, beta, None)
+        quantise_weight_piece(we_grouped, we_codes[:, 1, 1, :], we_scales[:, 1, 1, :])
+        e_banks = first_product(1)
+        wo_grouped = regroup_weight_piece(nc, w_grouped_pool, wo_raw[0], WO_SCALAR_COLS)
+        moments(12, 13)
+        normalise(1)
+        modulate(1)
+        quantise_weight_piece(wo_grouped, wo_codes[:, 0, :], wo_scales[:, 0, :])
+        out_of_banks(s_t, e_banks, None, c_bias)
+        c_banks = transpose_rows(nc, psum_t, s_t, l_t, ident)
+        for h in range(HALVES):
+            nc.scalar.copy(
+                out=c_rows[:, h * BANK : (h + 1) * BANK], in_=c_banks[h][:].rearrange("p i d -> p (i d)")
+            )
+        wo_grouped = regroup_weight_piece(nc, w_grouped_pool, wo_raw[1], WO_SCALAR_COLS)
+        moments(14, 15)
+        aggregate(15)
+        quantise_weight_piece(wo_grouped, wo_codes[:, 1, :], wo_scales[:, 1, :])
+        add_bias_to_residual(0)
+        prepare_scales(8)
+        make_scales(8)
+        normalise(2)
+
+        for t in range(T + MX_LAG):
+            if t < T:
+                transpose(t)
+                activate(t)
+            if t + 3 < T:
+                normalise(t + 3)
+            if t == 1:
+                prepare_scales(12)
+            if t >= MX_LAG:
+                project(t - MX_LAG)
+            if t + 2 < T:
+                modulate(t + 2)
+            if t >= MX_LAG:
+                finish(t - MX_LAG)
+            if t < T and t % GROUP == GROUP - 1:
+                quantise_group(t // GROUP)
+            if t == 3:
+                make_scales(12)
+            if t + 1 < T:
+                add_bias_to_residual(t + 1)

@@ -314,11 +314,7 @@ def tile_temporalcrossattention_pa_kernel(tc, x, y, emb0, We, be, ln2_g, ln2_b, 
 
         def add_bias_to_residual(t):
             x_bo[t] = x_bo_pool.tile([P, D], F32, tag="x_bo", name="x_bo")
-            for h in range(HALVES):
-                cols = slice(h * BANK, (h + 1) * BANK)
-                nc.gpsimd.tensor_tensor(
-                    out=x_bo[t][:, cols], in0=x_tiles[t][:, cols], in1=bo_rows[:, cols], op=ALU.add
-                )
+            nc.gpsimd.tensor_tensor(out=x_bo[t][:], in0=x_tiles[t], in1=bo_rows[:], op=ALU.add)
 
         def finish(t):
             res = res_pool.tile([P, D], F32, tag="res", name="res")

@@ -30,6 +30,7 @@ WO_SCALAR_COLS = 512
 X_TILES = 4
 BN_MAX = 512
 BN_DIM = 6
+WARM_UP = {1: 4, 2: 8, 3: 3}
 MX_LAG = 3
 
 FLOPS = 2 * P * D * (2 * D) + 2 * (P * T) * D * D
@@ -389,8 +390,11 @@ def tile_temporalcrossattention_pa_kernel(tc, x, y, emb0, We, be, ln2_g, ln2_b, 
         make_scales(8)
         normalise(2)
 
+        warm = psum_mm.tile([P, BANK], F32, tag="mm", name="warm")
         for t in range(T + MX_LAG):
             if t < T:
+                for i in range(WARM_UP.get(t, 0)):
+                    nc.tensor.matmul(out=warm[:], lhsT=ident_bf[:], rhs=bo_rows[:, 0:BANK], start=True, stop=True)
                 transpose(t)
                 activate(t)
             if t + 3 < T:

from contextlib import ExitStack

import concourse.mybir as mybir
from concourse.masks import make_identity

F32 = mybir.dt.float32
BF16 = mybir.dt.bfloat16
I32 = mybir.dt.int32
U32 = mybir.dt.uint32
U8 = mybir.dt.uint8
FP8X4 = mybir.dt.float8_e4m3fn_x4
ACT = mybir.ActivationFunctionType
ALU = mybir.AluOpType

P = 128
T = 16
D = 1024
EPS = 1e-5
PACK = 4
K_PASS = P * PACK
PASSES = D // K_PASS
CHUNKS = D // P
BANK = 512
HALVES = D // BANK
W_COLS = 1024
GROUP = 2
SCALES_TILES = 4
WE_SCALAR_COLS = 640
WO_SCALAR_COLS = 512
X_TILES = 4
BN_MAX = 512
BN_DIM = 6
WARM_UP = {1: 4, 2: 8, 3: 3}
MX_LAG = 3

FLOPS = 2 * P * D * (2 * D) + 2 * (P * T) * D * D


def load_weight_piece(nc, pool, rows):
    raw = pool.tile([P, PACK, W_COLS], BF16, tag="raw", name="raw")
    nc.sync.dma_start(out=raw[:], in_=rows.rearrange("(j p) n -> p j n", p=P))
    return raw


def regroup_weight_piece(nc, pool, raw, scalar_cols):
    grouped = pool.tile([P, W_COLS, PACK], BF16, align_bytes=64, name="grouped")
    nc.scalar.copy(
        out=grouped[:, 0:scalar_cols, :].rearrange("p (c i) j -> p c j i", i=4),
        in_=raw[:, :, 0:scalar_cols].rearrange("p j (c i) -> p c j i", i=4),
    )
    for first in range(scalar_cols, W_COLS, P):
        cols = slice(first, first + P)
        nc.gpsimd.tensor_scalar(
            out=grouped[:, cols, :],
            in0=raw[:, :, cols].rearrange("p j n -> p n j"),
            scalar1=1.0,
            scalar2=0.0,
            op0=ALU.mult,
            op1=ALU.add,
        )
    return grouped


def quantise(nc, grouped_flat, codes, scales):
    nc.vector.quantize_mx(out=codes.bitcast(FP8X4), scales=scales, in_=grouped_flat)


def transpose_rows(nc, psum, rows, addend, ident):
    banks = []
    for g in range(PASSES):
        bank = psum.tile([P, PACK, P], rows.dtype, tag="kT", name="kT")
        for j in range(PACK):
            cols = slice((PACK * g + j) * P, (PACK * g + j + 1) * P)
            if addend is None:
                nc.tensor.transpose(out=bank[:, j, :], in_=rows[:, cols], identity=ident[:])
            else:
                nc.tensor.matmul(
                    out=bank[:, j, :], lhsT=addend[:, cols], rhs=ident[:],
                    is_transpose=True, start=True, stop=False,
                )
                nc.tensor.matmul(
                    out=bank[:, j, :], lhsT=rows[:, cols], rhs=ident[:],
                    is_transpose=True, start=False, stop=True,
                )
        banks.append(bank)
    return banks


def silu_out_of_psum(nc, banks, grouped):
    for g in range(PASSES):
        nc.scalar.activation(
            out=grouped[:, g, :, :], in_=banks[g][:].rearrange("p j r -> p r j"), func=ACT.Silu
        )


def tile_temporalcrossattention_pa_kernel(tc, x, y, emb0, We, be, ln2_g, ln2_b, Wo, bo, out):
    nc = tc.nc
    with ExitStack() as ctx:
        keep = ctx.enter_context(tc.tile_pool(name="keep", bufs=1))
        we_raw_pool = ctx.enter_context(tc.tile_pool(name="we_raw", bufs=2 * PASSES))
        wo_raw_pool = ctx.enter_context(tc.tile_pool(name="wo_raw", bufs=PASSES))
        w_grouped_pool = ctx.enter_context(tc.tile_pool(name="w_grouped", bufs=2))
        z_pool = ctx.enter_context(tc.tile_pool(name="z", bufs=7))
        act_pool = ctx.enter_context(tc.tile_pool(name="act", bufs=3))
        res_pool = ctx.enter_context(tc.tile_pool(name="res", bufs=4))
        x_bo_pool = ctx.enter_context(tc.tile_pool(name="x_bo", bufs=6))
        small = ctx.enter_context(tc.tile_pool(name="small", bufs=4))
        psum_keep = ctx.enter_context(tc.psum_pool(name="psum_keep", bufs=HALVES))
        psum_t = ctx.enter_context(tc.psum_pool(name="psum_t", bufs=3))
        psum_mm = ctx.enter_context(tc.psum_pool(name="psum_mm", bufs=3))
        ctx.enter_context(tc.manual_schedule())

        vec_rows = keep.tile([P, P], BF16)
        nc.vector.memset(vec_rows[:].bitcast(I32), 0)
        ident = keep.tile([P, P], F32)
        make_identity(nc, ident[:])
        ident_bf = keep.tile([P, P], BF16)
        nc.vector.tensor_copy(out=ident_bf[:], in_=ident[:])
        minus_half = keep.tile([P, SCALES_TILES], F32)
        nc.gpsimd.memset(minus_half[:], -0.5)
        eps = keep.tile([P, 1], F32)
        nc.gpsimd.memset(eps[:], 0.0)
        nc.gpsimd.tensor_scalar(out=eps[:], in0=eps[:], scalar1=1.0, scalar2=EPS, op0=ALU.mult, op1=ALU.add)

        y_tiles = {}
        x_tiles = {}
        emb_raw = keep.tile([P, D], BF16)
        bo_rows = keep.tile([P, D], BF16)

        def load_y(lo, hi):
            part = keep.tile([P, hi - lo, D], BF16, name="y_%d" % lo)
            nc.sync.dma_start(out=part[:], in_=y[:, lo:hi, :])
            for t in range(lo, hi):
                y_tiles[t] = part[:, t - lo, :]

        def load_x(lo):
            part = we_raw_pool.tile([P, X_TILES, D], BF16, tag="raw", name="x_part")
            nc.sync.dma_start(out=part[:], in_=x[:, lo : lo + X_TILES, :])
            for t in range(lo, lo + X_TILES):
                x_tiles[t] = part[:, t - lo, :]

        def load_we(side, g):
            cols = slice(side * W_COLS, (side + 1) * W_COLS)
            return load_weight_piece(nc, we_raw_pool, We[g * K_PASS : (g + 1) * K_PASS, cols])

        def load_wo(g):
            return load_weight_piece(nc, wo_raw_pool, Wo[g * K_PASS : (g + 1) * K_PASS, :])

        load_y(0, 1)
        nc.sync.dma_start(out=emb_raw[:], in_=emb0)
        load_y(1, 2)
        nc.sync.dma_start(out=vec_rows[0:16, :], in_=be.rearrange("(r c) -> r c", c=P))
        nc.sync.dma_start(out=vec_rows[16:24, :], in_=ln2_g.rearrange("(r c) -> r c", c=P))
        nc.sync.dma_start(out=vec_rows[24:32, :], in_=ln2_b.rearrange("(r c) -> r c", c=P))
        load_y(2, 4)
        we_raw = {}
        we_raw[0, 0] = load_we(0, 0)
        load_y(4, 6)
        we_raw[0, 1] = load_we(0, 1)
        we_raw[1, 0] = load_we(1, 0)
        load_y(6, 8)
        we_raw[1, 1] = load_we(1, 1)
        load_y(8, 12)
        wo_raw = [load_wo(0)]
        load_y(12, 14)
        wo_raw.append(load_wo(1))
        load_y(14, 16)
        nc.sync.dma_start(out=bo_rows[:], in_=bo.partition_broadcast(P))

        emb_codes = keep.tile([P, PASSES, P], U32, align_bytes=64)
        emb_scales = keep.tile([P, PASSES, P], U8, align_bytes=64)
        we_codes = keep.tile([P, 2, PASSES, W_COLS], U32, align_bytes=64)
        we_scales = keep.tile([P, 2, PASSES, W_COLS], U8, align_bytes=64)
        wo_codes = keep.tile([P, PASSES, W_COLS], U32, align_bytes=64)
        wo_scales = keep.tile([P, PASSES, W_COLS], U8, align_bytes=64)
        mean_var = keep.tile([P, T, 2], F32)
        var_eps = keep.tile([P, T], F32)
        neg_mean = keep.tile([P, T], F32)
        rstd = keep.tile([P, T], F32)
        z_bias = keep.tile([P, T], F32)
        vec_cols = keep.tile([P, 4 * CHUNKS], F32)
        be_scale = vec_cols[:, 0:CHUNKS]
        be_shift = vec_cols[:, CHUNKS : 2 * CHUNKS]
        gain = vec_cols[:, 2 * CHUNKS : 3 * CHUNKS]
        beta = vec_cols[:, 3 * CHUNKS : 4 * CHUNKS]
        a_bias = keep.tile([P, CHUNKS], F32)
        c_bias = keep.tile([P, CHUNKS], F32)
        a_t = res_pool.tile([P, D], F32, tag="res", name="a_t")
        l_t = res_pool.tile([P, D], F32, tag="res", name="l_t")
        s_t = res_pool.tile([P, D], F32, tag="res", name="s_t")
        c_rows = keep.tile([P, D], F32)

        stats = {}

        def moments(*tiles):
            for t in tiles:
                stats[t] = small.tile([P, D // BN_MAX, BN_DIM], F32, name="stats")
                for s in range(D // BN_MAX):
                    nc.vector.bn_stats(out=stats[t][:, s, :], in_=y_tiles[t][:, s * BN_MAX : (s + 1) * BN_MAX])
                if t > 0:
                    aggregate(t - 1)

        def aggregate(t):
            nc.vector.bn_aggr(out=mean_var[:, t, :], in_=stats[t][:].rearrange("p s k -> p (s k)"))

        def prepare_scales(first):
            tiles = slice(first, first + SCALES_TILES)
            nc.scalar.activation(out=var_eps[:, tiles], in_=mean_var[:, tiles, 1], func=ACT.Identity, bias=eps[:])
            nc.scalar.mul(neg_mean[:, tiles], mean_var[:, tiles, 0], -1.0)

        def make_scales(first):
            tiles = slice(first, first + SCALES_TILES)
            nc.gpsimd.tensor_tensor(out=rstd[:, tiles], in0=var_eps[:, tiles], in1=minus_half[:], op=ALU.pow)

        def quantise_weight_piece(grouped, codes, scales):
            quantise(nc, grouped[:].rearrange("p n j -> p (n j)"), codes, scales)

        def first_product(side):
            banks = []
            for h in range(HALVES):
                bank = psum_mm.tile([P, PACK, P], F32, tag="mm", name="e_bank")
                for i in range(PACK):
                    cols = slice(h * BANK + i * P, h * BANK + (i + 1) * P)
                    for g in range(PASSES):
                        nc.tensor.matmul_mx(
                            out=bank[:, i, :],
                            lhsT=we_codes[:, side, g, cols].bitcast(FP8X4),
                            lhsT_scale=we_scales[:, side, g, cols],
                            rhs=emb_codes[:, g, :].bitcast(FP8X4),
                            rhs_scale=emb_scales[:, g, :],
                            start=(g == 0),
                            stop=(g == PASSES - 1),
                        )
                banks.append(bank)
            return banks

        def out_of_banks(table, banks, scale, bias):
            for k in range(CHUNKS):
                factors = {}
                if scale is not None:
                    factors["scale"] = scale[:, k : k + 1]
                if bias is not None:
                    factors["bias"] = bias[:, k : k + 1]
                nc.scalar.activation(
                    out=table[:, k * P : (k + 1) * P], in_=banks[k // PACK][:, k % PACK, :],
                    func=ACT.Identity, **factors,
                )

        z_tiles = {}
        h_banks = {}
        act_grouped = {}
        act_codes = {}
        act_scales = {}
        products = {}
        x_bo = {}

        def normalise(t):
            nc.scalar.activation(
                out=z_bias[:, t : t + 1], in_=neg_mean[:, t : t + 1], func=ACT.Identity, scale=rstd[:, t : t + 1]
            )
            z = z_pool.tile([P, D], F32, tag="z", name="z")
            nc.scalar.activation(
                out=z[:], in_=y_tiles[t], func=ACT.Identity, scale=rstd[:, t : t + 1], bias=z_bias[:, t : t + 1]
            )
            z_tiles[t] = z

        def modulate(t):
            z = z_tiles[t]
            for h in range(HALVES):
                cols = slice(h * BANK, (h + 1) * BANK)
                nc.vector.tensor_tensor(
                    out=z[:, cols], in0=z[:, cols], in1=a_banks[h][:].rearrange("p i d -> p (i d)"), op=ALU.mult
                )

        def transpose(t):
            h_banks[t] = transpose_rows(nc, psum_t, z_tiles[t], c_rows, ident)

        def activate(t):
            group, i = divmod(t, GROUP)
            if i == 0:
                act_grouped[group] = act_pool.tile(
                    [P, GROUP, PASSES, P, PACK], BF16, align_bytes=64, tag="act_grouped", name="act_grouped"
                )
            silu_out_of_psum(nc, h_banks[t], act_grouped[group][:, i, :, :, :])

        def quantise_group(group):
            codes = act_pool.tile([P, GROUP, PASSES, P], U32, align_bytes=64, tag="act_codes", name="act_codes")
            scales = act_pool.tile([P, GROUP, PASSES, P], U8, align_bytes=64, tag="act_scales", name="act_scales")
            quantise(
                nc,
                act_grouped[group][:].rearrange("p i g r j -> p (i g r j)"),
                codes[:].rearrange("p i g r -> p (i g r)"),
                scales[:].rearrange("p i g r -> p (i g r)"),
            )
            act_codes[group] = codes
            act_scales[group] = scales

        def project(t):
            group, i = divmod(t, GROUP)
            products[t] = []
            for h in range(HALVES):
                cols = slice(h * BANK, (h + 1) * BANK)
                acc = psum_mm.tile([P, BANK], F32, tag="mm", name="acc")
                for g in range(PASSES):
                    nc.tensor.matmul_mx(
                        out=acc[:],
                        lhsT=act_codes[group][:, i, g, :].bitcast(FP8X4),
                        lhsT_scale=act_scales[group][:, i, g, :],
                        rhs=wo_codes[:, g, cols].bitcast(FP8X4),
                        rhs_scale=wo_scales[:, g, cols],
                        start=(g == 0),
                        stop=(g == PASSES - 1),
                    )
                products[t].append(acc)

        def add_bias_to_residual(t):
            x_bo[t] = x_bo_pool.tile([P, D], F32, tag="x_bo", name="x_bo")
            nc.gpsimd.tensor_tensor(out=x_bo[t][:], in0=x_tiles[t], in1=bo_rows[:], op=ALU.add)

        def finish(t):
            res = res_pool.tile([P, D], F32, tag="res", name="res")
            for h in range(HALVES):
                cols = slice(h * BANK, (h + 1) * BANK)
                nc.vector.tensor_tensor(out=res[:, cols], in0=products[t][h][:], in1=x_bo[t][:, cols], op=ALU.add)
                if t == T - 1:
                    nc.sync.dma_start(out=out[:, t, cols], in_=res[:, cols])
            if t < T - 1:
                nc.sync.dma_start(out=out[:, t, :], in_=res[:])

        moments(0)
        emb_banks = transpose_rows(nc, psum_t, emb_raw, None, ident_bf)
        emb_grouped = act_pool.tile([P, PASSES, P, PACK], BF16, align_bytes=64, tag="emb_grouped", name="emb_grouped")
        silu_out_of_psum(nc, emb_banks, emb_grouped[:])
        quantise(
            nc,
            emb_grouped[:].rearrange("p g r j -> p (g r j)"),
            emb_codes[:].rearrange("p g r -> p (g r)"),
            emb_scales[:].rearrange("p g r -> p (g r)"),
        )
        vec_bank = psum_mm.tile([P, PACK, P], BF16, tag="mm", name="vec_bank")
        nc.tensor.transpose(out=vec_bank[:, 0, :], in_=vec_rows[:], identity=ident_bf[:])
        nc.vector.tensor_copy(out=vec_cols[:], in_=vec_bank[:, 0, 0 : 4 * CHUNKS])
        moments(1)
        nc.vector.scalar_tensor_tensor(out=a_bias[:], in0=be_scale, scalar=1.0, in1=gain, op0=ALU.add, op1=ALU.mult)
        nc.vector.scalar_tensor_tensor(out=c_bias[:], in0=be_scale, scalar=1.0, in1=beta, op0=ALU.add, op1=ALU.mult)
        nc.vector.tensor_tensor(out=c_bias[:], in0=c_bias[:], in1=be_shift, op=ALU.add)
        moments(2, 3, 4)

        we_grouped = regroup_weight_piece(nc, w_grouped_pool, we_raw[0, 0], WE_SCALAR_COLS)
        quantise_weight_piece(we_grouped, we_codes[:, 0, 0, :], we_scales[:, 0, 0, :])
        we_grouped = regroup_weight_piece(nc, w_grouped_pool, we_raw[0, 1], WE_SCALAR_COLS)
        moments(5, 6)
        quantise_weight_piece(we_grouped, we_codes[:, 0, 1, :], we_scales[:, 0, 1, :])
        e_banks = first_product(0)
        we_grouped = regroup_weight_piece(nc, w_grouped_pool, we_raw[1, 0], WE_SCALAR_COLS)
        prepare_scales(0)
        make_scales(0)
        moments(7, 8, 9)
        out_of_banks(a_t, e_banks, gain, a_bias)
        quantise_weight_piece(we_grouped, we_codes[:, 1, 0, :], we_scales[:, 1, 0, :])
        a_banks = transpose_rows(nc, psum_keep, a_t, None, ident)
        we_grouped = regroup_weight_piece(nc, w_grouped_pool, we_raw[1, 1], WE_SCALAR_COLS)
        prepare_scales(4)
        make_scales(4)
        for first in range(0, T, X_TILES):
            load_x(first)
        normalise(0)
        moments(10, 11)
        modulate(0)
        out_of_banks(l_t, e_banks, beta, None)
        quantise_weight_piece(we_grouped, we_codes[:, 1, 1, :], we_scales[:, 1, 1, :])
        e_banks = first_product(1)
        wo_grouped = regroup_weight_piece(nc, w_grouped_pool, wo_raw[0], WO_SCALAR_COLS)
        moments(12, 13)
        normalise(1)
        modulate(1)
        quantise_weight_piece(wo_grouped, wo_codes[:, 0, :], wo_scales[:, 0, :])
        out_of_banks(s_t, e_banks, None, c_bias)
        c_banks = transpose_rows(nc, psum_t, s_t, l_t, ident)
        for h in range(HALVES):
            nc.scalar.copy(
                out=c_rows[:, h * BANK : (h + 1) * BANK], in_=c_banks[h][:].rearrange("p i d -> p (i d)")
            )
        wo_grouped = regroup_weight_piece(nc, w_grouped_pool, wo_raw[1], WO_SCALAR_COLS)
        moments(14, 15)
        aggregate(15)
        quantise_weight_piece(wo_grouped, wo_codes[:, 1, :], wo_scales[:, 1, :])
        add_bias_to_residual(0)
        prepare_scales(8)
        make_scales(8)
        normalise(2)

        warm = psum_mm.tile([P, BANK], F32, tag="mm", name="warm")
        for t in range(T + MX_LAG):
            if t < T:
                for i in range(WARM_UP.get(t, 0)):
                    nc.tensor.matmul(out=warm[:], lhsT=ident_bf[:], rhs=bo_rows[:, 0:BANK], start=True, stop=True)
                transpose(t)
                activate(t)
            if t + 3 < T:
                normalise(t + 3)
            if t == 1:
                prepare_scales(12)
            if t >= MX_LAG:
                project(t - MX_LAG)
            if t + 2 < T:
                modulate(t + 2)
            if t >= MX_LAG:
                finish(t - MX_LAG)
            if t < T and t % GROUP == GROUP - 1:
                quantise_group(t // GROUP)
            if t == 3:
                make_scales(12)
            if t + 1 < T:
                add_bias_to_residual(t + 1)
